import numpy as np
import ml_dtypes


def mxq(x, axis, fmt="e4m3"):
    dtype, down = {"e4m3": (ml_dtypes.float8_e4m3fn, 7), "e5m2": (ml_dtypes.float8_e5m2, 14)}[fmt]
    v = np.moveaxis(np.asarray(x, np.float32).astype(ml_dtypes.bfloat16).astype(np.float64), axis, -1)
    blocks = v.reshape(v.shape[:-1] + (-1, 32))
    amax = np.abs(blocks).max(-1, keepdims=True)
    byte = np.maximum(np.where(amax > 0, np.frexp(amax)[1] - 1 + 127, 0) - down, 1)
    scale = np.exp2(byte - 127.0)
    codes = (blocks / scale).astype(np.float32).astype(dtype).astype(np.float64)
    return np.moveaxis((codes * scale).reshape(v.shape), -1, axis)


WIDE = False


def mx_kscale(k):
    if not WIDE:
        return np.ones(k)
    levels = np.array([10, -10, 5, -5, 0])
    a = np.random.permutation(np.resize(levels, k // 512 * 4)).reshape(k // 512, 4)
    idx = np.arange(k)
    return np.exp2(a[idx // 512, idx % 128 // 32])


BF16 = ml_dtypes.bfloat16


def bf(x):
    return np.asarray(x, np.float32).astype(BF16)


def f64(x):
    return np.asarray(x).astype(np.float64)


B, S, H, U, A = 4, 4096, 1024, 128, 128
NEG = -1e20


def setup_inputs():
    s = mx_kscale(S)
    h = np.tanh(np.random.standard_normal((B, S, U)))
    h[:, :, 0] = 0.25 * h[:, :, 0] - np.log2(s)[None, :] / 16.0
    w = np.random.standard_normal((U, A)) * 5.0 / np.sqrt(U)
    w[0, :] = 16.0 * np.log(2.0)
    return {"h_tanh": bf(h),
            "W2": bf(w),
            "padding_mask": bf(np.random.random((B, S)) < 0.75),
            "data": bf(np.random.standard_normal((B, S, H)) * 5.0 * s[None, :, None] * np.mean(1.0 / s))}


def reference(h_tanh, W2, padding_mask, data):
    logits = f64(h_tanh) @ f64(W2)
    m = f64(padding_mask)[:, :, None]
    logits = logits * m + (1.0 - m) * NEG
    e = np.exp(logits - logits.max(axis=1, keepdims=True))
    attended = (mxq(e, 1, "e4m3").transpose(0, 2, 1) @ mxq(f64(data), 1, "e4m3")) / e.sum(axis=1)[:, :, None]
    return attended.mean(axis=1)

@@ -1,0 +1,202 @@
+from contextlib import ExitStack
+
+import concourse.mybir as mybir
+from concourse.masks import make_identity
+
+BF16 = mybir.dt.bfloat16
+F32 = mybir.dt.float32
+U32 = mybir.dt.uint32
+U8 = mybir.dt.uint8
+FP8X4 = mybir.dt.float8_e4m3fn_x4
+ALU = mybir.AluOpType
+ACT = mybir.ActivationFunctionType
+AX = mybir.AxisListType
+
+B, S, H, U, A = 4, 4096, 1024, 128, 128
+P = 128
+PACK = 4
+K_PASS = P * PACK
+PASSES = S // K_PASS
+N_TILE = 512
+N_TILES = H // N_TILE
+NEG = -1e20
+EXP_COLS = 2 * K_PASS
+EXP_PIECES = S // EXP_COLS
+RUN = 4
+V_COLS = 544
+
+FLOPS = 2 * B * S * U * A + 2 * B * S * A * H
+
+
+def tile_selfattentionpooling_pa_kernel(tc, h_tanh, W2, padding_mask, data, out):
+    nc = tc.nc
+    with ExitStack() as ctx:
+        const = ctx.enter_context(tc.tile_pool(name="const", bufs=1))
+        h_pool = ctx.enter_context(tc.tile_pool(name="h", bufs=2))
+        stage = ctx.enter_context(tc.tile_pool(name="stage", bufs=3))
+        score_pool = ctx.enter_context(tc.tile_pool(name="scores", bufs=2))
+        small = ctx.enter_context(tc.tile_pool(name="small", bufs=3))
+        e_keep = ctx.enter_context(tc.tile_pool(name="e_keep", bufs=2))
+        raw_pool = ctx.enter_context(tc.tile_pool(name="raw", bufs=4))
+        grp_pool = ctx.enter_context(tc.tile_pool(name="grouped", bufs=3))
+        d_keep = ctx.enter_context(tc.tile_pool(name="d_keep", bufs=8))
+        fin = ctx.enter_context(tc.tile_pool(name="fin", bufs=2))
+        psum = ctx.enter_context(tc.psum_pool(name="psum", bufs=1))
+
+        ident_bf = const.tile([P, P], BF16)
+        make_identity(nc, ident_bf[:])
+        ident_f32 = const.tile([P, P], F32)
+        make_identity(nc, ident_f32[:])
+        mean_w = const.tile([A, P], F32)
+        nc.vector.memset(mean_w[:], 1.0 / A)
+        w2_sb = const.tile([U, A], BF16)
+        nc.sync.dma_start(out=w2_sb[:], in_=W2)
+
+        mask_cols = const.tile([P, B * PASSES, PACK], BF16)
+        nc.scalar.dma_start(
+            out=mask_cols[:], in_=padding_mask.rearrange("b (c p t) -> p (b c) t", p=P, t=PACK)
+        )
+        pad_term = const.tile([P, B * PASSES, PACK], F32)
+        nc.vector.tensor_scalar(
+            out=pad_term[:], in0=mask_cols[:], scalar1=1.0, scalar2=-NEG, op0=ALU.subtract, op1=ALU.mult
+        )
+
+        def load_h(b):
+            h_nat = h_pool.tile([P, PASSES, PACK, U], BF16, name="h_nat")
+            nc.sync.dma_start(
+                out=h_nat[:].rearrange("p c t u -> p c (t u)"),
+                in_=h_tanh[b].rearrange("(c p t) u -> p c (t u)", p=P, t=PACK),
+            )
+            return h_nat
+
+        def attention_weights(b, h_nat):
+            scores = score_pool.tile([A, S], F32, name="scores")
+            chunk_max = small.tile([A, PASSES], F32, name="chunk_max")
+            for c in range(PASSES):
+                hT_ps = psum.tile([U, PACK, P], BF16, tag="hT", bufs=2, name="hT_ps")
+                for t in range(PACK):
+                    nc.tensor.transpose(hT_ps[:, t, :], h_nat[:, c, t, :], ident_bf[:])
+                hT = stage.tile([U, PACK, P], BF16, name="hT")
+                nc.scalar.copy(out=hT[:], in_=hT_ps[:])
+                l_ps = psum.tile([A, PACK, P], F32, tag="l", bufs=2, name="l_ps")
+                for t in range(PACK):
+                    nc.tensor.matmul(
+                        out=l_ps[:, t, :],
+                        lhsT=pad_term[:, b * PASSES + c, t : t + 1].to_broadcast([P, A]),
+                        rhs=ident_f32[:],
+                        is_transpose=True,
+                        start=(t == 0),
+                        stop=False,
+                    )
+                nc.tensor.matmul(
+                    out=l_ps[:].rearrange("a t p -> a (t p)"),
+                    lhsT=w2_sb[:],
+                    rhs=hT[:].rearrange("u t p -> u (t p)"),
+                    start=False,
+                    stop=True,
+                )
+                nc.vector.tensor_scalar(
+                    out=scores[:, c * K_PASS : (c + 1) * K_PASS].rearrange("a (p t) -> a p t", t=PACK),
+                    in0=l_ps[:].rearrange("a t p -> a p t"),
+                    scalar1=1.0,
+                    scalar2=None,
+                    op0=ALU.mult,
+                    op1=ALU.max,
+                    accum_out=chunk_max[:, c : c + 1],
+                )
+            col_max = small.tile([A, 1], F32, name="col_max")
+            nc.vector.tensor_reduce(out=col_max[:], in_=chunk_max[:], axis=AX.X, op=ALU.max)
+            neg_max = small.tile([A, 1], F32, name="neg_max")
+            nc.vector.tensor_scalar_mul(out=neg_max[:], in0=col_max[:], scalar1=-1.0)
+
+            e_T = score_pool.tile([A, S], BF16, name="e_T")
+            sum_parts = small.tile([A, EXP_PIECES], F32, name="sum_parts")
+            for i in range(EXP_PIECES):
+                cols = slice(i * EXP_COLS, (i + 1) * EXP_COLS)
+                nc.scalar.activation(
+                    out=e_T[:, cols],
+                    in_=scores[:, cols],
+                    func=ACT.Exp,
+                    bias=neg_max[:, 0:1],
+                    scale=1.0,
+                    accum_out=sum_parts[:, i : i + 1],
+                )
+            col_sum = small.tile([A, 1], F32, name="col_sum")
+            nc.vector.tensor_reduce(out=col_sum[:], in_=sum_parts[:], axis=AX.X, op=ALU.add)
+            inv_sum = e_keep.tile([A, 1], F32, name="inv_sum")
+            nc.vector.reciprocal(out=inv_sum[:], in_=col_sum[:])
+
+            e_words = e_T[:].bitcast(F32)
+            e_grouped = score_pool.tile([P, PASSES, A, PACK], BF16, name="e_grouped", bufs=1, align_bytes=64)
+            for i in range(PASSES // 2):
+                eW_ps = psum.tile([P, 2, 2, A], F32, tag="eW", bufs=1, name="eW_ps")
+                for gg in range(2):
+                    for u in range(2):
+                        w0 = ((2 * i + gg) * 2 + u) * P
+                        nc.tensor.transpose(eW_ps[:, gg, u, :], e_words[:, w0 : w0 + P], ident_f32[:])
+                nc.scalar.copy(
+                    out=e_grouped[:, 2 * i : 2 * i + 2, :, :].bitcast(F32),
+                    in_=eW_ps[:].rearrange("p g u a -> p g a u"),
+                )
+            e_codes = e_keep.tile([P, PASSES, A], U32, name="e_codes", align_bytes=64)
+            e_scales = e_keep.tile([P, PASSES, A], U8, name="e_scales", align_bytes=64)
+            nc.vector.quantize_mx(
+                out=e_codes[:].rearrange("p g a -> p (g a)").bitcast(FP8X4),
+                scales=e_scales[:].rearrange("p g a -> p (g a)"),
+                in_=e_grouped[:].rearrange("p g a j -> p (g a j)"),
+            )
+            return e_codes, e_scales, inv_sum
+
+        def regroup(copy, raw, grouped, h0, h1):
+            copy(
+                out=grouped[:, h0:h1, :].rearrange("p (c i) j -> p c j i", i=RUN),
+                in_=raw[:, :, h0:h1].rearrange("p j (c i) -> p c j i", i=RUN),
+            )
+
+        def quantise_data(b, g):
+            raw = raw_pool.tile([P, PACK, H], BF16, name="raw")
+            nc.sync.dma_start(
+                out=raw[:].rearrange("p (u e) h -> p u (e h)", e=2),
+                in_=data[b, g * K_PASS : (g + 1) * K_PASS, :].rearrange("(u p e) h -> p u (e h)", u=2, e=2),
+            )
+            grouped = grp_pool.tile([P, H, PACK], BF16, name="grouped", align_bytes=64)
+            regroup(nc.vector.tensor_copy, raw, grouped, 0, V_COLS)
+            regroup(nc.scalar.copy, raw, grouped, V_COLS, H)
+            d_codes = d_keep.tile([P, H], U32, name="d_codes", align_bytes=64)
+            d_scales = d_keep.tile([P, H], U8, name="d_scales", align_bytes=64)
+            nc.vector.quantize_mx(
+                out=d_codes[:].bitcast(FP8X4),
+                scales=d_scales[:],
+                in_=grouped[:].rearrange("p h j -> p (h j)"),
+            )
+            return d_codes, d_scales
+
+        weights = {0: attention_weights(0, load_h(0))}
+        for b in range(B):
+            if b + 1 < B:
+                weights[b + 1] = attention_weights(b + 1, load_h(b + 1))
+            e_codes, e_scales, inv_sum = weights[b]
+            acc = [psum.tile([A, N_TILE], F32, tag="acc%d" % n, name="acc%d" % n) for n in range(N_TILES)]
+            for g in range(PASSES):
+                d_codes, d_scales = quantise_data(b, g)
+                for n in range(N_TILES):
+                    cols = slice(n * N_TILE, (n + 1) * N_TILE)
+                    nc.tensor.matmul_mx(
+                        out=acc[n][:],
+                        lhsT=e_codes[:, g, :].bitcast(FP8X4),
+                        lhsT_scale=e_scales[:, g, :],
+                        rhs=d_codes[:, cols].bitcast(FP8X4),
+                        rhs_scale=d_scales[:, cols],
+                        start=(g == 0),
+                        stop=(g == PASSES - 1),
+                    )
+            attended = fin.tile([A, H], F32, name="attended")
+            nc.vector.tensor_scalar_mul(out=attended[:, 0:N_TILE], in0=acc[0][:], scalar1=inv_sum[:, 0:1])
+            nc.scalar.activation(out=attended[:, N_TILE:H], in_=acc[1][:], func=ACT.Copy, scale=inv_sum[:, 0:1])
+            pooled = fin.tile([P, H], F32, name="pooled")
+            for n in range(N_TILES):
+                cols = slice(n * N_TILE, (n + 1) * N_TILE)
+                mean_ps = psum.tile([P, N_TILE], F32, tag="mean", name="mean_ps")
+                nc.tensor.matmul(out=mean_ps[:], lhsT=mean_w[:], rhs=attended[:, cols], start=True, stop=True)
+                nc.scalar.copy(out=pooled[:, cols], in_=mean_ps[:])
+            nc.sync.dma_start(out=out[b : b + 1, :], in_=pooled[0:1, :])

@@ -16,187 +16,291 @@ B, S, H, U, A = 4, 4096, 1024, 128, 128
 P = 128
 PACK = 4
 K_PASS = P * PACK
-PASSES = S // K_PASS
+SEQ_PASSES = S // K_PASS
+ALL_PASSES = B * SEQ_PASSES
 N_TILE = 512
 N_TILES = H // N_TILE
 NEG = -1e20
-EXP_COLS = 2 * K_PASS
-EXP_PIECES = S // EXP_COLS
+UNIT_PASSES = 2
+UNIT = UNIT_PASSES * K_PASS
+SEQ_UNITS = S // UNIT
+ALL_UNITS = B * SEQ_UNITS
 RUN = 4
 V_COLS = 544
 
+LOAD_AHEAD = 3
+H_AHEAD = 2
+QUANTISE_LAG = 2
+MULTIPLY_LAG = 3
+SCORE_LAG = 1
+DRAIN_LAG = 2
+EXP_LAG = 5
+E_TRANSPOSE_LAG = 6
+E_QUANTISE_LAG = 7
+E_READY_LAG = 8
+SCORE_BANKS_FREE = ALL_UNITS + DRAIN_LAG + 1
+
 FLOPS = 2 * B * S * U * A + 2 * B * S * A * H
+
+
+def multiply_slot(j):
+    return max(j + MULTIPLY_LAG, j // UNIT_PASSES + E_READY_LAG)
+
+
+def scale_slot(b):
+    return multiply_slot((b + 1) * SEQ_PASSES - 1)
+
+
+def mean_slot(b):
+    return max(scale_slot(b) + 1, SCORE_BANKS_FREE + b)
 
 
 def tile_selfattentionpooling_pa_kernel(tc, h_tanh, W2, padding_mask, data, out):
     nc = tc.nc
     with ExitStack() as ctx:
+        ctx.enter_context(tc.manual_schedule())
         const = ctx.enter_context(tc.tile_pool(name="const", bufs=1))
         h_pool = ctx.enter_context(tc.tile_pool(name="h", bufs=2))
-        stage = ctx.enter_context(tc.tile_pool(name="stage", bufs=3))
-        score_pool = ctx.enter_context(tc.tile_pool(name="scores", bufs=2))
-        small = ctx.enter_context(tc.tile_pool(name="small", bufs=3))
-        e_keep = ctx.enter_context(tc.tile_pool(name="e_keep", bufs=2))
+        stage = ctx.enter_context(tc.tile_pool(name="stage", bufs=2))
+        seq_pool = ctx.enter_context(tc.tile_pool(name="seq", bufs=2))
+        small = ctx.enter_context(tc.tile_pool(name="small", bufs=B))
         raw_pool = ctx.enter_context(tc.tile_pool(name="raw", bufs=4))
-        grp_pool = ctx.enter_context(tc.tile_pool(name="grouped", bufs=3))
+        grp_pool = ctx.enter_context(tc.tile_pool(name="grouped", bufs=4))
         d_keep = ctx.enter_context(tc.tile_pool(name="d_keep", bufs=8))
-        fin = ctx.enter_context(tc.tile_pool(name="fin", bufs=2))
+        fin = ctx.enter_context(tc.tile_pool(name="fin", bufs=B))
         psum = ctx.enter_context(tc.psum_pool(name="psum", bufs=1))
 
-        ident_bf = const.tile([P, P], BF16)
-        make_identity(nc, ident_bf[:])
-        ident_f32 = const.tile([P, P], F32)
-        make_identity(nc, ident_f32[:])
-        mean_w = const.tile([A, P], F32)
-        nc.vector.memset(mean_w[:], 1.0 / A)
-        w2_sb = const.tile([U, A], BF16)
-        nc.sync.dma_start(out=w2_sb[:], in_=W2)
+        h_nat, scores, chunk_max, neg_max, e_T, sum_parts, inv_sum, acc, attended = ({} for n in range(9))
+        hT_ps, hT, l_ps, eW_ps, e_grouped = ({} for n in range(5))
+        raw, grouped, d_codes, d_scales = ({} for n in range(4))
+        mean_ps = []
 
-        mask_cols = const.tile([P, B * PASSES, PACK], BF16)
-        nc.scalar.dma_start(
-            out=mask_cols[:], in_=padding_mask.rearrange("b (c p t) -> p (b c) t", p=P, t=PACK)
-        )
-        pad_term = const.tile([P, B * PASSES, PACK], F32)
-        nc.vector.tensor_scalar(
-            out=pad_term[:], in0=mask_cols[:], scalar1=1.0, scalar2=-NEG, op0=ALU.subtract, op1=ALU.mult
-        )
+        def load_data(i):
+            b, g = divmod(i, SEQ_PASSES)
+            raw[i] = raw_pool.tile([P, PACK, H], BF16, name="raw")
+            nc.sync.dma_start(
+                out=raw[i][:].rearrange("p (u e) h -> p u (e h)", e=2),
+                in_=data[b, g * K_PASS : (g + 1) * K_PASS, :].rearrange("(u p e) h -> p u (e h)", u=2, e=2),
+            )
 
         def load_h(b):
-            h_nat = h_pool.tile([P, PASSES, PACK, U], BF16, name="h_nat")
+            h_nat[b] = h_pool.tile([P, SEQ_PASSES, PACK, U], BF16, name="h_nat")
             nc.sync.dma_start(
-                out=h_nat[:].rearrange("p c t u -> p c (t u)"),
+                out=h_nat[b][:].rearrange("p c t u -> p c (t u)"),
                 in_=h_tanh[b].rearrange("(c p t) u -> p c (t u)", p=P, t=PACK),
             )
-            return h_nat
 
-        def attention_weights(b, h_nat):
-            scores = score_pool.tile([A, S], F32, name="scores")
-            chunk_max = small.tile([A, PASSES], F32, name="chunk_max")
-            for c in range(PASSES):
-                hT_ps = psum.tile([U, PACK, P], BF16, tag="hT", bufs=2, name="hT_ps")
-                for t in range(PACK):
-                    nc.tensor.transpose(hT_ps[:, t, :], h_nat[:, c, t, :], ident_bf[:])
-                hT = stage.tile([U, PACK, P], BF16, name="hT")
-                nc.scalar.copy(out=hT[:], in_=hT_ps[:])
-                l_ps = psum.tile([A, PACK, P], F32, tag="l", bufs=2, name="l_ps")
+        def padding_terms(u):
+            for cc in range(UNIT_PASSES):
+                l_ps[u, cc] = psum.tile([A, PACK, P], F32, tag="l", bufs=4, name="l_ps")
                 for t in range(PACK):
                     nc.tensor.matmul(
-                        out=l_ps[:, t, :],
-                        lhsT=pad_term[:, b * PASSES + c, t : t + 1].to_broadcast([P, A]),
+                        out=l_ps[u, cc][:, t, :],
+                        lhsT=pad_term[:, u * UNIT_PASSES + cc, t : t + 1].to_broadcast([P, A]),
                         rhs=ident_f32[:],
                         is_transpose=True,
                         start=(t == 0),
                         stop=False,
                     )
+
+        def transpose_h(u):
+            b, r = divmod(u, SEQ_UNITS)
+            hT_ps[u] = psum.tile([U, UNIT_PASSES, PACK, P], BF16, tag="hT", name="hT_ps")
+            for cc in range(UNIT_PASSES):
+                for t in range(PACK):
+                    nc.tensor.transpose(hT_ps[u][:, cc, t, :], h_nat[b][:, r * UNIT_PASSES + cc, t, :], ident_bf[:])
+
+        def copy_hT(u):
+            hT[u] = stage.tile([U, UNIT_PASSES, PACK, P], BF16, name="hT")
+            nc.scalar.copy(out=hT[u][:], in_=hT_ps[u][:])
+
+        def score_matmuls(u):
+            for cc in range(UNIT_PASSES):
                 nc.tensor.matmul(
-                    out=l_ps[:].rearrange("a t p -> a (t p)"),
+                    out=l_ps[u, cc][:].rearrange("a t p -> a (t p)"),
                     lhsT=w2_sb[:],
-                    rhs=hT[:].rearrange("u t p -> u (t p)"),
+                    rhs=hT[u][:, cc, :, :].rearrange("u t p -> u (t p)"),
                     start=False,
                     stop=True,
                 )
+
+        def drain_scores(u):
+            b, r = divmod(u, SEQ_UNITS)
+            if r == 0:
+                scores[b] = seq_pool.tile([A, S], F32, name="scores")
+                chunk_max[b] = small.tile([A, SEQ_PASSES], F32, name="chunk_max")
+            for cc in range(UNIT_PASSES):
+                c = r * UNIT_PASSES + cc
                 nc.vector.tensor_scalar(
-                    out=scores[:, c * K_PASS : (c + 1) * K_PASS].rearrange("a (p t) -> a p t", t=PACK),
-                    in0=l_ps[:].rearrange("a t p -> a p t"),
+                    out=scores[b][:, c * K_PASS : (c + 1) * K_PASS].rearrange("a (p t) -> a p t", t=PACK),
+                    in0=l_ps[u, cc][:].rearrange("a t p -> a p t"),
                     scalar1=1.0,
                     scalar2=None,
                     op0=ALU.mult,
                     op1=ALU.max,
-                    accum_out=chunk_max[:, c : c + 1],
+                    accum_out=chunk_max[b][:, c : c + 1],
                 )
-            col_max = small.tile([A, 1], F32, name="col_max")
-            nc.vector.tensor_reduce(out=col_max[:], in_=chunk_max[:], axis=AX.X, op=ALU.max)
-            neg_max = small.tile([A, 1], F32, name="neg_max")
-            nc.vector.tensor_scalar_mul(out=neg_max[:], in0=col_max[:], scalar1=-1.0)
+            if r == SEQ_UNITS - 1:
+                col_max = small.tile([A, 1], F32, name="col_max")
+                nc.vector.tensor_reduce(out=col_max[:], in_=chunk_max[b][:], axis=AX.X, op=ALU.max)
+                neg_max[b] = small.tile([A, 1], F32, name="neg_max")
+                nc.vector.tensor_scalar_mul(out=neg_max[b][:], in0=col_max[:], scalar1=-1.0)
 
-            e_T = score_pool.tile([A, S], BF16, name="e_T")
-            sum_parts = small.tile([A, EXP_PIECES], F32, name="sum_parts")
-            for i in range(EXP_PIECES):
-                cols = slice(i * EXP_COLS, (i + 1) * EXP_COLS)
-                nc.scalar.activation(
-                    out=e_T[:, cols],
-                    in_=scores[:, cols],
-                    func=ACT.Exp,
-                    bias=neg_max[:, 0:1],
-                    scale=1.0,
-                    accum_out=sum_parts[:, i : i + 1],
-                )
+        def exponentials(k):
+            b, r = divmod(k, SEQ_UNITS)
+            if r == 0:
+                e_T[b] = seq_pool.tile([A, S], BF16, name="e_T")
+                sum_parts[b] = small.tile([A, SEQ_UNITS], F32, name="sum_parts")
+            cols = slice(r * UNIT, (r + 1) * UNIT)
+            nc.scalar.activation(
+                out=e_T[b][:, cols],
+                in_=scores[b][:, cols],
+                func=ACT.Exp,
+                bias=neg_max[b][:, 0:1],
+                scale=1.0,
+                accum_out=sum_parts[b][:, r : r + 1],
+            )
+
+        def invert_sum(b):
             col_sum = small.tile([A, 1], F32, name="col_sum")
-            nc.vector.tensor_reduce(out=col_sum[:], in_=sum_parts[:], axis=AX.X, op=ALU.add)
-            inv_sum = e_keep.tile([A, 1], F32, name="inv_sum")
-            nc.vector.reciprocal(out=inv_sum[:], in_=col_sum[:])
+            nc.vector.tensor_reduce(out=col_sum[:], in_=sum_parts[b][:], axis=AX.X, op=ALU.add)
+            inv_sum[b] = small.tile([A, 1], F32, name="inv_sum")
+            nc.vector.reciprocal(out=inv_sum[b][:], in_=col_sum[:])
 
-            e_words = e_T[:].bitcast(F32)
-            e_grouped = score_pool.tile([P, PASSES, A, PACK], BF16, name="e_grouped", bufs=1, align_bytes=64)
-            for i in range(PASSES // 2):
-                eW_ps = psum.tile([P, 2, 2, A], F32, tag="eW", bufs=1, name="eW_ps")
-                for gg in range(2):
-                    for u in range(2):
-                        w0 = ((2 * i + gg) * 2 + u) * P
-                        nc.tensor.transpose(eW_ps[:, gg, u, :], e_words[:, w0 : w0 + P], ident_f32[:])
-                nc.scalar.copy(
-                    out=e_grouped[:, 2 * i : 2 * i + 2, :, :].bitcast(F32),
-                    in_=eW_ps[:].rearrange("p g u a -> p g a u"),
+        def transpose_e(k):
+            b, r = divmod(k, SEQ_UNITS)
+            e_words = e_T[b][:].bitcast(F32)
+            eW_ps[k] = psum.tile([P, UNIT_PASSES, 2, A], F32, tag="eW", name="eW_ps")
+            for gg in range(UNIT_PASSES):
+                for u in range(2):
+                    w0 = ((r * UNIT_PASSES + gg) * 2 + u) * P
+                    nc.tensor.transpose(eW_ps[k][:, gg, u, :], e_words[:, w0 : w0 + P], ident_f32[:])
+
+        def copy_e(k):
+            e_grouped[k] = stage.tile([P, UNIT_PASSES, A, PACK], BF16, name="e_grouped", align_bytes=64)
+            nc.scalar.copy(out=e_grouped[k][:].bitcast(F32), in_=eW_ps[k][:].rearrange("p g u a -> p g a u"))
+
+        def quantise_e(k):
+            passes = slice(k * UNIT_PASSES, (k + 1) * UNIT_PASSES)
+            nc.vector.quantize_mx(
+                out=e_codes[:, passes, :].rearrange("p g a -> p (g a)").bitcast(FP8X4),
+                scales=e_scales[:, passes, :].rearrange("p g a -> p (g a)"),
+                in_=e_grouped[k][:].rearrange("p g a j -> p (g a j)"),
+            )
+
+        def regroup(i):
+            grouped[i] = grp_pool.tile([P, H, PACK], BF16, name="grouped", align_bytes=64)
+            for copy, h0, h1 in ((nc.vector.tensor_copy, 0, V_COLS), (nc.scalar.copy, V_COLS, H)):
+                copy(
+                    out=grouped[i][:, h0:h1, :].rearrange("p (c i) j -> p c j i", i=RUN),
+                    in_=raw[i][:, :, h0:h1].rearrange("p j (c i) -> p c j i", i=RUN),
                 )
-            e_codes = e_keep.tile([P, PASSES, A], U32, name="e_codes", align_bytes=64)
-            e_scales = e_keep.tile([P, PASSES, A], U8, name="e_scales", align_bytes=64)
+
+        def quantise_data(i):
+            d_codes[i] = d_keep.tile([P, H], U32, name="d_codes", align_bytes=64)
+            d_scales[i] = d_keep.tile([P, H], U8, name="d_scales", align_bytes=64)
             nc.vector.quantize_mx(
-                out=e_codes[:].rearrange("p g a -> p (g a)").bitcast(FP8X4),
-                scales=e_scales[:].rearrange("p g a -> p (g a)"),
-                in_=e_grouped[:].rearrange("p g a j -> p (g a j)"),
-            )
-            return e_codes, e_scales, inv_sum
-
-        def regroup(copy, raw, grouped, h0, h1):
-            copy(
-                out=grouped[:, h0:h1, :].rearrange("p (c i) j -> p c j i", i=RUN),
-                in_=raw[:, :, h0:h1].rearrange("p j (c i) -> p c j i", i=RUN),
+                out=d_codes[i][:].bitcast(FP8X4),
+                scales=d_scales[i][:],
+                in_=grouped[i][:].rearrange("p h j -> p (h j)"),
             )
 
-        def quantise_data(b, g):
-            raw = raw_pool.tile([P, PACK, H], BF16, name="raw")
-            nc.sync.dma_start(
-                out=raw[:].rearrange("p (u e) h -> p u (e h)", e=2),
-                in_=data[b, g * K_PASS : (g + 1) * K_PASS, :].rearrange("(u p e) h -> p u (e h)", u=2, e=2),
-            )
-            grouped = grp_pool.tile([P, H, PACK], BF16, name="grouped", align_bytes=64)
-            regroup(nc.vector.tensor_copy, raw, grouped, 0, V_COLS)
-            regroup(nc.scalar.copy, raw, grouped, V_COLS, H)
-            d_codes = d_keep.tile([P, H], U32, name="d_codes", align_bytes=64)
-            d_scales = d_keep.tile([P, H], U8, name="d_scales", align_bytes=64)
-            nc.vector.quantize_mx(
-                out=d_codes[:].bitcast(FP8X4),
-                scales=d_scales[:],
-                in_=grouped[:].rearrange("p h j -> p (h j)"),
-            )
-            return d_codes, d_scales
-
-        weights = {0: attention_weights(0, load_h(0))}
-        for b in range(B):
-            if b + 1 < B:
-                weights[b + 1] = attention_weights(b + 1, load_h(b + 1))
-            e_codes, e_scales, inv_sum = weights[b]
-            acc = [psum.tile([A, N_TILE], F32, tag="acc%d" % n, name="acc%d" % n) for n in range(N_TILES)]
-            for g in range(PASSES):
-                d_codes, d_scales = quantise_data(b, g)
-                for n in range(N_TILES):
-                    cols = slice(n * N_TILE, (n + 1) * N_TILE)
-                    nc.tensor.matmul_mx(
-                        out=acc[n][:],
-                        lhsT=e_codes[:, g, :].bitcast(FP8X4),
-                        lhsT_scale=e_scales[:, g, :],
-                        rhs=d_codes[:, cols].bitcast(FP8X4),
-                        rhs_scale=d_scales[:, cols],
-                        start=(g == 0),
-                        stop=(g == PASSES - 1),
-                    )
-            attended = fin.tile([A, H], F32, name="attended")
-            nc.vector.tensor_scalar_mul(out=attended[:, 0:N_TILE], in0=acc[0][:], scalar1=inv_sum[:, 0:1])
-            nc.scalar.activation(out=attended[:, N_TILE:H], in_=acc[1][:], func=ACT.Copy, scale=inv_sum[:, 0:1])
-            pooled = fin.tile([P, H], F32, name="pooled")
+        def multiply(j):
+            b, g = divmod(j, SEQ_PASSES)
+            if g == 0:
+                acc[b] = [psum.tile([A, N_TILE], F32, tag="acc%d" % n, name="acc%d" % n) for n in range(N_TILES)]
             for n in range(N_TILES):
                 cols = slice(n * N_TILE, (n + 1) * N_TILE)
-                mean_ps = psum.tile([P, N_TILE], F32, tag="mean", name="mean_ps")
-                nc.tensor.matmul(out=mean_ps[:], lhsT=mean_w[:], rhs=attended[:, cols], start=True, stop=True)
-                nc.scalar.copy(out=pooled[:, cols], in_=mean_ps[:])
-            nc.sync.dma_start(out=out[b : b + 1, :], in_=pooled[0:1, :])
+                nc.tensor.matmul_mx(
+                    out=acc[b][n][:],
+                    lhsT=e_codes[:, j, :].bitcast(FP8X4),
+                    lhsT_scale=e_scales[:, j, :],
+                    rhs=d_codes[j][:, cols].bitcast(FP8X4),
+                    rhs_scale=d_scales[j][:, cols],
+                    start=(g == 0),
+                    stop=(g == SEQ_PASSES - 1),
+                )
+
+        def scale(b):
+            attended[b] = fin.tile([A, H], F32, name="attended")
+            nc.vector.tensor_scalar_mul(out=attended[b][:, 0:N_TILE], in0=acc[b][0][:], scalar1=inv_sum[b][:, 0:1])
+            nc.scalar.activation(
+                out=attended[b][:, N_TILE:H], in_=acc[b][1][:], func=ACT.Copy, scale=inv_sum[b][:, 0:1]
+            )
+
+        def head_mean(b):
+            for n in range(N_TILES):
+                if b == 0:
+                    mean_ps.append(psum.tile([P, N_TILE], F32, tag="l", bufs=4, name="mean_ps"))
+                nc.tensor.matmul(
+                    out=mean_ps[n][:],
+                    lhsT=select_w[:, b, :],
+                    rhs=attended[b][:, n * N_TILE : (n + 1) * N_TILE],
+                    start=(b == 0),
+                    stop=(b == B - 1),
+                )
+
+        def at(run_stage, index, count):
+            if 0 <= index < count:
+                run_stage(index)
+
+        w2_sb = const.tile([U, A], BF16)
+        nc.scalar.dma_start(out=w2_sb[:], in_=W2)
+        mask_cols = const.tile([P, ALL_PASSES, PACK], BF16)
+        nc.scalar.dma_start(
+            out=mask_cols[:], in_=padding_mask.rearrange("b (c p t) -> p (b c) t", p=P, t=PACK)
+        )
+        load_data(0)
+        load_h(0)
+        for i in range(1, LOAD_AHEAD):
+            load_data(i)
+
+        ident_bf = const.tile([P, P], BF16)
+        make_identity(nc, ident_bf[:])
+        ident_f32 = const.tile([P, P], F32)
+        make_identity(nc, ident_f32[:])
+        select_w = const.tile([A, B, P], F32)
+        nc.vector.memset(select_w[:], 0.0)
+        for b in range(B):
+            nc.vector.memset(select_w[:, b, b : b + 1], 1.0 / A)
+        pad_term = const.tile([P, ALL_PASSES, PACK], F32)
+        nc.vector.tensor_scalar(
+            out=pad_term[:], in0=mask_cols[:], scalar1=1.0, scalar2=-NEG, op0=ALU.subtract, op1=ALU.mult
+        )
+        e_codes = const.tile([P, ALL_PASSES, A], U32, align_bytes=64)
+        e_scales = const.tile([P, ALL_PASSES, A], U8, align_bytes=64)
+
+        for slot in range(mean_slot(B - 1) + 1):
+            at(load_data, slot + LOAD_AHEAD, ALL_PASSES)
+            if (slot + H_AHEAD) % SEQ_UNITS == 0:
+                at(load_h, (slot + H_AHEAD) // SEQ_UNITS, B)
+
+            at(copy_hT, slot - SCORE_LAG, ALL_UNITS)
+            at(copy_e, slot - E_QUANTISE_LAG, ALL_UNITS)
+
+            for j in range(ALL_PASSES):
+                if multiply_slot(j) == slot:
+                    multiply(j)
+            at(score_matmuls, slot - SCORE_LAG, ALL_UNITS)
+            for b in range(B):
+                if mean_slot(b) == slot:
+                    head_mean(b)
+            at(padding_terms, slot, ALL_UNITS)
+            at(transpose_h, slot, ALL_UNITS)
+            at(transpose_e, slot - E_TRANSPOSE_LAG, ALL_UNITS)
+
+            at(drain_scores, slot - DRAIN_LAG, ALL_UNITS)
+            if (slot - E_TRANSPOSE_LAG) % SEQ_UNITS == SEQ_UNITS - 1:
+                at(invert_sum, (slot - E_TRANSPOSE_LAG) // SEQ_UNITS, B)
+            at(regroup, slot, ALL_PASSES)
+            at(quantise_data, slot - QUANTISE_LAG, ALL_PASSES)
+            at(exponentials, slot - EXP_LAG, ALL_UNITS)
+            at(quantise_e, slot - E_QUANTISE_LAG, ALL_UNITS)
+            for b in range(B):
+                if scale_slot(b) == slot:
+                    scale(b)
+
+        pooled = fin.tile([P, H], F32, name="pooled")
+        nc.vector.tensor_copy(out=pooled[:, 0:N_TILE], in_=mean_ps[0][:])
+        nc.scalar.copy(out=pooled[:, N_TILE:H], in_=mean_ps[1][:])
+        nc.sync.dma_start(out=out, in_=pooled[0:B, :])

@@ -26,7 +26,7 @@ UNIT = UNIT_PASSES * K_PASS
 SEQ_UNITS = S // UNIT
 ALL_UNITS = B * SEQ_UNITS
 RUN = 4
-V_COLS = 544
+V_COLS = 560
 
 LOAD_AHEAD = 3
 H_AHEAD = 2
@@ -34,17 +34,24 @@ QUANTISE_LAG = 2
 MULTIPLY_LAG = 3
 SCORE_LAG = 1
 DRAIN_LAG = 2
-EXP_LAG = 5
-E_TRANSPOSE_LAG = 6
-E_QUANTISE_LAG = 7
-E_READY_LAG = 8
-SCORE_BANKS_FREE = ALL_UNITS + DRAIN_LAG + 1
+EXP_LAG = 6
+E_TRANSPOSE_LAG = 7
+E_QUANTISE_LAG = 8
+E_READY_LAG = 9
 
 FLOPS = 2 * B * S * U * A + 2 * B * S * A * H
 
 
+def unit_slot(u):
+    return 3 * u // 2
+
+
+def units_due(slot, lag):
+    return [u for u in range(ALL_UNITS) if unit_slot(u) + lag == slot]
+
+
 def multiply_slot(j):
-    return max(j + MULTIPLY_LAG, j // UNIT_PASSES + E_READY_LAG)
+    return max(j + MULTIPLY_LAG, unit_slot(j // UNIT_PASSES) + E_READY_LAG)
 
 
 def scale_slot(b):
@@ -52,7 +59,7 @@ def scale_slot(b):
 
 
 def mean_slot(b):
-    return max(scale_slot(b) + 1, SCORE_BANKS_FREE + b)
+    return max(scale_slot(b) + 1, unit_slot(ALL_UNITS - 1) + DRAIN_LAG + 1 + b)
 
 
 def tile_selfattentionpooling_pa_kernel(tc, h_tanh, W2, padding_mask, data, out):
@@ -70,7 +77,7 @@ def tile_selfattentionpooling_pa_kernel(tc, h_tanh, W2, padding_mask, data, out)
         fin = ctx.enter_context(tc.tile_pool(name="fin", bufs=B))
         psum = ctx.enter_context(tc.psum_pool(name="psum", bufs=1))
 
-        h_nat, scores, chunk_max, neg_max, e_T, sum_parts, inv_sum, acc, attended = ({} for n in range(9))
+        h_nat, scores, chunk_max, neg_max, e_T, sum_parts, acc, attended = ({} for n in range(8))
         hT_ps, hT, l_ps, eW_ps, e_grouped = ({} for n in range(5))
         raw, grouped, d_codes, d_scales = ({} for n in range(4))
         mean_ps = []
@@ -161,12 +168,6 @@ def tile_selfattentionpooling_pa_kernel(tc, h_tanh, W2, padding_mask, data, out)
                 accum_out=sum_parts[b][:, r : r + 1],
             )
 
-        def invert_sum(b):
-            col_sum = small.tile([A, 1], F32, name="col_sum")
-            nc.vector.tensor_reduce(out=col_sum[:], in_=sum_parts[b][:], axis=AX.X, op=ALU.add)
-            inv_sum[b] = small.tile([A, 1], F32, name="inv_sum")
-            nc.vector.reciprocal(out=inv_sum[b][:], in_=col_sum[:])
-
         def transpose_e(k):
             b, r = divmod(k, SEQ_UNITS)
             e_words = e_T[b][:].bitcast(F32)
@@ -222,11 +223,13 @@ def tile_selfattentionpooling_pa_kernel(tc, h_tanh, W2, padding_mask, data, out)
                 )
 
         def scale(b):
+            col_sum = small.tile([A, 1], F32, name="col_sum")
+            nc.vector.tensor_reduce(out=col_sum[:], in_=sum_parts[b][:], axis=AX.X, op=ALU.add)
+            inv_sum = small.tile([A, 1], F32, name="inv_sum")
+            nc.vector.reciprocal(out=inv_sum[:], in_=col_sum[:])
             attended[b] = fin.tile([A, H], F32, name="attended")
-            nc.vector.tensor_scalar_mul(out=attended[b][:, 0:N_TILE], in0=acc[b][0][:], scalar1=inv_sum[b][:, 0:1])
-            nc.scalar.activation(
-                out=attended[b][:, N_TILE:H], in_=acc[b][1][:], func=ACT.Copy, scale=inv_sum[b][:, 0:1]
-            )
+            nc.vector.tensor_scalar_mul(out=attended[b][:, 0:N_TILE], in0=acc[b][0][:], scalar1=inv_sum[:, 0:1])
+            nc.scalar.activation(out=attended[b][:, N_TILE:H], in_=acc[b][1][:], func=ACT.Copy, scale=inv_sum[:, 0:1])
 
         def head_mean(b):
             for n in range(N_TILES):
@@ -240,16 +243,11 @@ def tile_selfattentionpooling_pa_kernel(tc, h_tanh, W2, padding_mask, data, out)
                     stop=(b == B - 1),
                 )
 
-        def at(run_stage, index, count):
-            if 0 <= index < count:
-                run_stage(index)
-
         w2_sb = const.tile([U, A], BF16)
         nc.scalar.dma_start(out=w2_sb[:], in_=W2)
-        mask_cols = const.tile([P, ALL_PASSES, PACK], BF16)
-        nc.scalar.dma_start(
-            out=mask_cols[:], in_=padding_mask.rearrange("b (c p t) -> p (b c) t", p=P, t=PACK)
-        )
+        mask_rows = const.tile([P, K_PASS], BF16)
+        nc.vector.memset(mask_rows[:], 0.0)
+        nc.scalar.dma_start(out=mask_rows[0:ALL_PASSES, :], in_=padding_mask.rearrange("b (c k) -> (b c) k", k=K_PASS))
         load_data(0)
         load_h(0)
         for i in range(1, LOAD_AHEAD):
@@ -263,44 +261,62 @@ def tile_selfattentionpooling_pa_kernel(tc, h_tanh, W2, padding_mask, data, out)
         nc.vector.memset(select_w[:], 0.0)
         for b in range(B):
             nc.vector.memset(select_w[:, b, b : b + 1], 1.0 / A)
+        mask_ps = psum.tile([P, PACK, P], BF16, tag="hT", name="mask_ps")
+        for t in range(PACK):
+            nc.tensor.transpose(mask_ps[:, t, :], mask_rows[:].rearrange("r (p t) -> r t p", t=PACK)[:, t, :], ident_bf[:])
         pad_term = const.tile([P, ALL_PASSES, PACK], F32)
         nc.vector.tensor_scalar(
-            out=pad_term[:], in0=mask_cols[:], scalar1=1.0, scalar2=-NEG, op0=ALU.subtract, op1=ALU.mult
+            out=pad_term[:],
+            in0=mask_ps[:, :, 0:ALL_PASSES].rearrange("p t r -> p r t"),
+            scalar1=1.0,
+            scalar2=-NEG,
+            op0=ALU.subtract,
+            op1=ALU.mult,
         )
         e_codes = const.tile([P, ALL_PASSES, A], U32, align_bytes=64)
         e_scales = const.tile([P, ALL_PASSES, A], U8, align_bytes=64)
 
         for slot in range(mean_slot(B - 1) + 1):
-            at(load_data, slot + LOAD_AHEAD, ALL_PASSES)
-            if (slot + H_AHEAD) % SEQ_UNITS == 0:
-                at(load_h, (slot + H_AHEAD) // SEQ_UNITS, B)
+            if slot + LOAD_AHEAD < ALL_PASSES:
+                load_data(slot + LOAD_AHEAD)
+            for b in range(1, B):
+                if unit_slot(b * SEQ_UNITS) - H_AHEAD == slot:
+                    load_h(b)
 
-            at(copy_hT, slot - SCORE_LAG, ALL_UNITS)
-            at(copy_e, slot - E_QUANTISE_LAG, ALL_UNITS)
+            for u in units_due(slot, SCORE_LAG):
+                copy_hT(u)
+            for k in units_due(slot, E_QUANTISE_LAG):
+                copy_e(k)
 
             for j in range(ALL_PASSES):
                 if multiply_slot(j) == slot:
                     multiply(j)
-            at(score_matmuls, slot - SCORE_LAG, ALL_UNITS)
+            for u in units_due(slot, SCORE_LAG):
+                score_matmuls(u)
             for b in range(B):
                 if mean_slot(b) == slot:
                     head_mean(b)
-            at(padding_terms, slot, ALL_UNITS)
-            at(transpose_h, slot, ALL_UNITS)
-            at(transpose_e, slot - E_TRANSPOSE_LAG, ALL_UNITS)
+            for u in units_due(slot, 0):
+                padding_terms(u)
+                transpose_h(u)
+            for k in units_due(slot, E_TRANSPOSE_LAG):
+                transpose_e(k)
 
-            at(drain_scores, slot - DRAIN_LAG, ALL_UNITS)
-            if (slot - E_TRANSPOSE_LAG) % SEQ_UNITS == SEQ_UNITS - 1:
-                at(invert_sum, (slot - E_TRANSPOSE_LAG) // SEQ_UNITS, B)
-            at(regroup, slot, ALL_PASSES)
-            at(quantise_data, slot - QUANTISE_LAG, ALL_PASSES)
-            at(exponentials, slot - EXP_LAG, ALL_UNITS)
-            at(quantise_e, slot - E_QUANTISE_LAG, ALL_UNITS)
+            for u in units_due(slot, DRAIN_LAG):
+                drain_scores(u)
+            if slot < ALL_PASSES:
+                regroup(slot)
+            if 0 <= slot - QUANTISE_LAG < ALL_PASSES:
+                quantise_data(slot - QUANTISE_LAG)
+            for k in units_due(slot, EXP_LAG):
+                exponentials(k)
+            for k in units_due(slot, E_QUANTISE_LAG):
+                quantise_e(k)
             for b in range(B):
                 if scale_slot(b) == slot:
                     scale(b)
 
-        pooled = fin.tile([P, H], F32, name="pooled")
+        pooled = fin.tile([P, H], F32, name="pooled", bufs=1)
         nc.vector.tensor_copy(out=pooled[:, 0:N_TILE], in_=mean_ps[0][:])
         nc.scalar.copy(out=pooled[:, N_TILE:H], in_=mean_ps[1][:])
         nc.sync.dma_start(out=out, in_=pooled[0:B, :])

@@ -18,26 +18,26 @@ PACK = 4
 K_PASS = P * PACK
 SEQ_PASSES = S // K_PASS
 ALL_PASSES = B * SEQ_PASSES
-N_TILE = 512
-N_TILES = H // N_TILE
+LAST = ALL_PASSES - 1
 NEG = -1e20
 UNIT_PASSES = 2
 UNIT = UNIT_PASSES * K_PASS
 SEQ_UNITS = S // UNIT
 ALL_UNITS = B * SEQ_UNITS
 RUN = 4
-V_COLS = 560
+HALF = H // 2
+QUARTER = H // 4
 
 LOAD_AHEAD = 3
-H_AHEAD = 2
+H_AHEAD = 3
 QUANTISE_LAG = 2
 MULTIPLY_LAG = 3
 SCORE_LAG = 1
 DRAIN_LAG = 2
-EXP_LAG = 6
-E_TRANSPOSE_LAG = 7
-E_QUANTISE_LAG = 8
-E_READY_LAG = 9
+EXP_LAG = 7
+E_TRANSPOSE_LAG = 8
+E_QUANTISE_LAG = 9
+E_READY_LAG = 10
 
 FLOPS = 2 * B * S * U * A + 2 * B * S * A * H
 
@@ -54,12 +54,13 @@ def multiply_slot(j):
     return max(j + MULTIPLY_LAG, unit_slot(j // UNIT_PASSES) + E_READY_LAG)
 
 
-def scale_slot(b):
-    return multiply_slot((b + 1) * SEQ_PASSES - 1)
+def vector_columns(i):
+    return 432 if i < EXP_LAG else 560
 
 
-def mean_slot(b):
-    return max(scale_slot(b) + 1, unit_slot(ALL_UNITS - 1) + DRAIN_LAG + 1 + b)
+def parts(b):
+    width = QUARTER if b == B - 1 else HALF
+    return [slice(h, h + width) for h in range(0, H, width)]
 
 
 def tile_selfattentionpooling_pa_kernel(tc, h_tanh, W2, padding_mask, data, out):
@@ -67,35 +68,50 @@ def tile_selfattentionpooling_pa_kernel(tc, h_tanh, W2, padding_mask, data, out)
     with ExitStack() as ctx:
         ctx.enter_context(tc.manual_schedule())
         const = ctx.enter_context(tc.tile_pool(name="const", bufs=1))
-        h_pool = ctx.enter_context(tc.tile_pool(name="h", bufs=2))
+        h_pool = ctx.enter_context(tc.tile_pool(name="h", bufs=5))
         stage = ctx.enter_context(tc.tile_pool(name="stage", bufs=2))
         seq_pool = ctx.enter_context(tc.tile_pool(name="seq", bufs=2))
         small = ctx.enter_context(tc.tile_pool(name="small", bufs=B))
         raw_pool = ctx.enter_context(tc.tile_pool(name="raw", bufs=4))
         grp_pool = ctx.enter_context(tc.tile_pool(name="grouped", bufs=4))
-        d_keep = ctx.enter_context(tc.tile_pool(name="d_keep", bufs=8))
-        fin = ctx.enter_context(tc.tile_pool(name="fin", bufs=B))
+        d_keep = ctx.enter_context(tc.tile_pool(name="d_keep", bufs=10))
+        fin = ctx.enter_context(tc.tile_pool(name="fin", bufs=2))
         psum = ctx.enter_context(tc.psum_pool(name="psum", bufs=1))
 
-        h_nat, scores, chunk_max, neg_max, e_T, sum_parts, acc, attended = ({} for n in range(8))
+        h_nat, scores, chunk_max, neg_max, e_T, sum_parts, inv_sum = ({} for n in range(7))
         hT_ps, hT, l_ps, eW_ps, e_grouped = ({} for n in range(5))
-        raw, grouped, d_codes, d_scales = ({} for n in range(4))
-        mean_ps = []
+        raw, grouped, d_codes, d_scales, acc, attended, mean_ps, pooled = ({} for n in range(8))
 
-        def load_data(i):
+        def load_data(i, cols=slice(0, H)):
             b, g = divmod(i, SEQ_PASSES)
-            raw[i] = raw_pool.tile([P, PACK, H], BF16, name="raw")
+            if i not in raw:
+                raw[i] = raw_pool.tile([P, PACK, H], BF16, name="raw")
+            src = data[b, g * K_PASS : (g + 1) * K_PASS, :]
+            if cols == slice(0, H):
+                nc.sync.dma_start(
+                    out=raw[i][:].rearrange("p (u e) h -> p u (e h)", e=2),
+                    in_=src.rearrange("(u p e) h -> p u (e h)", u=2, e=2),
+                )
+            else:
+                for u in range(2):
+                    nc.sync.dma_start(
+                        out=raw[i][:, 2 * u : 2 * u + 2, cols],
+                        in_=src.rearrange("(u p e) h -> u p e h", u=2, e=2)[u, :, :, cols],
+                    )
+
+        def load_h(u):
+            b, r = divmod(u, SEQ_UNITS)
+            h_nat[u] = h_pool.tile([P, UNIT_PASSES, PACK, U], BF16, name="h_nat")
             nc.sync.dma_start(
-                out=raw[i][:].rearrange("p (u e) h -> p u (e h)", e=2),
-                in_=data[b, g * K_PASS : (g + 1) * K_PASS, :].rearrange("(u p e) h -> p u (e h)", u=2, e=2),
+                out=h_nat[u][:].rearrange("p c t u -> p c (t u)"),
+                in_=h_tanh[b, r * UNIT : (r + 1) * UNIT, :].rearrange("(c p t) u -> p c (t u)", p=P, t=PACK),
             )
 
-        def load_h(b):
-            h_nat[b] = h_pool.tile([P, SEQ_PASSES, PACK, U], BF16, name="h_nat")
-            nc.sync.dma_start(
-                out=h_nat[b][:].rearrange("p c t u -> p c (t u)"),
-                in_=h_tanh[b].rearrange("(c p t) u -> p c (t u)", p=P, t=PACK),
-            )
+        def transpose_h(u):
+            hT_ps[u] = psum.tile([U, UNIT_PASSES, PACK, P], BF16, tag="hT", name="hT_ps")
+            for cc in range(UNIT_PASSES):
+                for t in range(PACK):
+                    nc.tensor.transpose(hT_ps[u][:, cc, t, :], h_nat[u][:, cc, t, :], ident_bf[:])
 
         def padding_terms(u):
             for cc in range(UNIT_PASSES):
@@ -109,13 +125,6 @@ def tile_selfattentionpooling_pa_kernel(tc, h_tanh, W2, padding_mask, data, out)
                         start=(t == 0),
                         stop=False,
                     )
-
-        def transpose_h(u):
-            b, r = divmod(u, SEQ_UNITS)
-            hT_ps[u] = psum.tile([U, UNIT_PASSES, PACK, P], BF16, tag="hT", name="hT_ps")
-            for cc in range(UNIT_PASSES):
-                for t in range(PACK):
-                    nc.tensor.transpose(hT_ps[u][:, cc, t, :], h_nat[b][:, r * UNIT_PASSES + cc, t, :], ident_bf[:])
 
         def copy_hT(u):
             hT[u] = stage.tile([U, UNIT_PASSES, PACK, P], BF16, name="hT")
@@ -147,11 +156,12 @@ def tile_selfattentionpooling_pa_kernel(tc, h_tanh, W2, padding_mask, data, out)
                     op1=ALU.max,
                     accum_out=chunk_max[b][:, c : c + 1],
                 )
-            if r == SEQ_UNITS - 1:
-                col_max = small.tile([A, 1], F32, name="col_max")
-                nc.vector.tensor_reduce(out=col_max[:], in_=chunk_max[b][:], axis=AX.X, op=ALU.max)
-                neg_max[b] = small.tile([A, 1], F32, name="neg_max")
-                nc.vector.tensor_scalar_mul(out=neg_max[b][:], in0=col_max[:], scalar1=-1.0)
+
+        def score_max(b):
+            col_max = small.tile([A, 1], F32, name="col_max")
+            nc.vector.tensor_reduce(out=col_max[:], in_=chunk_max[b][:], axis=AX.X, op=ALU.max)
+            neg_max[b] = small.tile([A, 1], F32, name="neg_max")
+            nc.vector.tensor_scalar_mul(out=neg_max[b][:], in0=col_max[:], scalar1=-1.0)
 
         def exponentials(k):
             b, r = divmod(k, SEQ_UNITS)
@@ -189,134 +199,195 @@ def tile_selfattentionpooling_pa_kernel(tc, h_tanh, W2, padding_mask, data, out)
                 in_=e_grouped[k][:].rearrange("p g a j -> p (g a j)"),
             )
 
-        def regroup(i):
-            grouped[i] = grp_pool.tile([P, H, PACK], BF16, name="grouped", align_bytes=64)
-            for copy, h0, h1 in ((nc.vector.tensor_copy, 0, V_COLS), (nc.scalar.copy, V_COLS, H)):
+        def regroup(i, cols, v_cols):
+            if i not in grouped:
+                grouped[i] = grp_pool.tile([P, H, PACK], BF16, name="grouped", align_bytes=64)
+            middle = cols.start + v_cols
+            for copy, h0, h1 in ((nc.vector.tensor_copy, cols.start, middle), (nc.scalar.copy, middle, cols.stop)):
                 copy(
                     out=grouped[i][:, h0:h1, :].rearrange("p (c i) j -> p c j i", i=RUN),
                     in_=raw[i][:, :, h0:h1].rearrange("p j (c i) -> p c j i", i=RUN),
                 )
 
-        def quantise_data(i):
-            d_codes[i] = d_keep.tile([P, H], U32, name="d_codes", align_bytes=64)
-            d_scales[i] = d_keep.tile([P, H], U8, name="d_scales", align_bytes=64)
+        def quantise_data(i, cols=slice(0, H)):
+            if i not in d_codes:
+                d_codes[i] = d_keep.tile([P, H], U32, name="d_codes", align_bytes=64)
+                d_scales[i] = d_keep.tile([P, H], U8, name="d_scales", align_bytes=64)
             nc.vector.quantize_mx(
-                out=d_codes[i][:].bitcast(FP8X4),
-                scales=d_scales[i][:],
-                in_=grouped[i][:].rearrange("p h j -> p (h j)"),
+                out=d_codes[i][:, cols].bitcast(FP8X4),
+                scales=d_scales[i][:, cols],
+                in_=grouped[i][:, cols, :].rearrange("p h j -> p (h j)"),
             )
 
-        def multiply(j):
+        def multiply(j, n):
             b, g = divmod(j, SEQ_PASSES)
+            cols = parts(b)[n]
             if g == 0:
-                acc[b] = [psum.tile([A, N_TILE], F32, tag="acc%d" % n, name="acc%d" % n) for n in range(N_TILES)]
-            for n in range(N_TILES):
-                cols = slice(n * N_TILE, (n + 1) * N_TILE)
-                nc.tensor.matmul_mx(
-                    out=acc[b][n][:],
-                    lhsT=e_codes[:, j, :].bitcast(FP8X4),
-                    lhsT_scale=e_scales[:, j, :],
-                    rhs=d_codes[j][:, cols].bitcast(FP8X4),
-                    rhs_scale=d_scales[j][:, cols],
-                    start=(g == 0),
-                    stop=(g == SEQ_PASSES - 1),
-                )
+                tag, bufs = ("l", 4) if b == B - 1 else ("acc%d" % n, 1)
+                acc[b, n] = psum.tile([A, cols.stop - cols.start], F32, tag=tag, bufs=bufs, name="acc")
+            nc.tensor.matmul_mx(
+                out=acc[b, n][:],
+                lhsT=e_codes[:, j, :].bitcast(FP8X4),
+                lhsT_scale=e_scales[:, j, :],
+                rhs=d_codes[j][:, cols].bitcast(FP8X4),
+                rhs_scale=d_scales[j][:, cols],
+                start=(g == 0),
+                stop=(g == SEQ_PASSES - 1),
+            )
 
-        def scale(b):
+        def invert_sums(b):
             col_sum = small.tile([A, 1], F32, name="col_sum")
             nc.vector.tensor_reduce(out=col_sum[:], in_=sum_parts[b][:], axis=AX.X, op=ALU.add)
-            inv_sum = small.tile([A, 1], F32, name="inv_sum")
-            nc.vector.reciprocal(out=inv_sum[:], in_=col_sum[:])
-            attended[b] = fin.tile([A, H], F32, name="attended")
-            nc.vector.tensor_scalar_mul(out=attended[b][:, 0:N_TILE], in0=acc[b][0][:], scalar1=inv_sum[:, 0:1])
-            nc.scalar.activation(out=attended[b][:, N_TILE:H], in_=acc[b][1][:], func=ACT.Copy, scale=inv_sum[:, 0:1])
+            inv_sum[b] = small.tile([A, 1], F32, name="inv_sum")
+            nc.vector.reciprocal(out=inv_sum[b][:], in_=col_sum[:])
 
-        def head_mean(b):
-            for n in range(N_TILES):
-                if b == 0:
-                    mean_ps.append(psum.tile([P, N_TILE], F32, tag="l", bufs=4, name="mean_ps"))
-                nc.tensor.matmul(
-                    out=mean_ps[n][:],
-                    lhsT=select_w[:, b, :],
-                    rhs=attended[b][:, n * N_TILE : (n + 1) * N_TILE],
-                    start=(b == 0),
-                    stop=(b == B - 1),
-                )
+        def take_product(b, n, copy):
+            if n == 0:
+                attended[b] = fin.tile([A, H], F32, name="attended")
+            copy(out=attended[b][:, parts(b)[n]], in_=acc[b, n][:])
+
+        def head_mean(b, n):
+            cols = parts(b)[n]
+            tag = ("acc0", "acc1", "hT", "eW")[n]
+            mean_ps[b, n] = psum.tile([P, cols.stop - cols.start], F32, tag=tag, name="mean_ps")
+            nc.tensor.matmul(
+                out=mean_ps[b, n][:],
+                lhsT=inv_sum[b][:, 0:1].to_broadcast([A, P]),
+                rhs=attended[b][:, cols],
+                start=True,
+                stop=True,
+            )
+
+        def take_mean(b, n, on_vector):
+            if n == 0:
+                pooled[b] = fin.tile([1, H], F32, name="pooled")
+            dst = pooled[b][:, parts(b)[n]]
+            if on_vector:
+                nc.vector.tensor_scalar_mul(out=dst, in0=mean_ps[b, n][0:1, :], scalar1=1.0 / A)
+            else:
+                nc.scalar.mul(dst, mean_ps[b, n][0:1, :], 1.0 / A)
+
+        def store(b):
+            nc.sync.dma_start(out=out[b : b + 1, :], in_=pooled[b][:])
 
         w2_sb = const.tile([U, A], BF16)
         nc.scalar.dma_start(out=w2_sb[:], in_=W2)
         mask_rows = const.tile([P, K_PASS], BF16)
         nc.vector.memset(mask_rows[:], 0.0)
         nc.scalar.dma_start(out=mask_rows[0:ALL_PASSES, :], in_=padding_mask.rearrange("b (c k) -> (b c) k", k=K_PASS))
-        load_data(0)
+        load_data(0, slice(0, HALF))
+        load_data(0, slice(HALF, H))
         load_h(0)
-        for i in range(1, LOAD_AHEAD):
-            load_data(i)
+        load_data(1)
+        load_h(1)
+        load_data(2)
 
         ident_bf = const.tile([P, P], BF16)
         make_identity(nc, ident_bf[:])
         ident_f32 = const.tile([P, P], F32)
         make_identity(nc, ident_f32[:])
-        select_w = const.tile([A, B, P], F32)
-        nc.vector.memset(select_w[:], 0.0)
-        for b in range(B):
-            nc.vector.memset(select_w[:, b, b : b + 1], 1.0 / A)
-        mask_ps = psum.tile([P, PACK, P], BF16, tag="hT", name="mask_ps")
-        for t in range(PACK):
-            nc.tensor.transpose(mask_ps[:, t, :], mask_rows[:].rearrange("r (p t) -> r t p", t=PACK)[:, t, :], ident_bf[:])
         pad_term = const.tile([P, ALL_PASSES, PACK], F32)
-        nc.vector.tensor_scalar(
-            out=pad_term[:],
-            in0=mask_ps[:, :, 0:ALL_PASSES].rearrange("p t r -> p r t"),
-            scalar1=1.0,
-            scalar2=-NEG,
-            op0=ALU.subtract,
-            op1=ALU.mult,
-        )
         e_codes = const.tile([P, ALL_PASSES, A], U32, align_bytes=64)
         e_scales = const.tile([P, ALL_PASSES, A], U8, align_bytes=64)
 
-        for slot in range(mean_slot(B - 1) + 1):
+        def mask_terms():
+            mask_ps = psum.tile([P, PACK, P], BF16, tag="eW", name="mask_ps")
+            for t in range(PACK):
+                nc.tensor.transpose(mask_ps[:, t, :], mask_rows[:].rearrange("r (p t) -> r t p", t=PACK)[:, t, :], ident_bf[:])
+            nc.vector.tensor_scalar(
+                out=pad_term[:],
+                in0=mask_ps[:, :, 0:ALL_PASSES].rearrange("p t r -> p r t"),
+                scalar1=1.0,
+                scalar2=-NEG,
+                op0=ALU.subtract,
+                op1=ALU.mult,
+            )
+
+        for slot in range(ALL_PASSES - 1):
             if slot + LOAD_AHEAD < ALL_PASSES:
                 load_data(slot + LOAD_AHEAD)
-            for b in range(1, B):
-                if unit_slot(b * SEQ_UNITS) - H_AHEAD == slot:
-                    load_h(b)
+            for u in units_due(slot, -H_AHEAD):
+                if u > 1:
+                    load_h(u)
 
             for u in units_due(slot, SCORE_LAG):
                 copy_hT(u)
             for k in units_due(slot, E_QUANTISE_LAG):
                 copy_e(k)
 
+            for b in range(B - 1):
+                if multiply_slot((b + 1) * SEQ_PASSES - 1) + 1 == slot:
+                    for n in range(len(parts(b))):
+                        head_mean(b, n)
             for j in range(ALL_PASSES):
                 if multiply_slot(j) == slot:
-                    multiply(j)
+                    for n in range(len(parts(j // SEQ_PASSES))):
+                        multiply(j, n)
             for u in units_due(slot, SCORE_LAG):
                 score_matmuls(u)
-            for b in range(B):
-                if mean_slot(b) == slot:
-                    head_mean(b)
-            for u in units_due(slot, 0):
-                padding_terms(u)
-                transpose_h(u)
+            if slot == 0:
+                regroup(0, slice(0, HALF), 256)
+                regroup(0, slice(HALF, H), 256)
+                transpose_h(0)
+                mask_terms()
+                padding_terms(0)
+            else:
+                for u in units_due(slot, 0):
+                    transpose_h(u)
+                    padding_terms(u)
             for k in units_due(slot, E_TRANSPOSE_LAG):
                 transpose_e(k)
 
             for u in units_due(slot, DRAIN_LAG):
                 drain_scores(u)
-            if slot < ALL_PASSES:
-                regroup(slot)
-            if 0 <= slot - QUANTISE_LAG < ALL_PASSES:
+            if slot > 0:
+                regroup(slot, slice(0, H), vector_columns(slot))
+            for u in units_due(slot, DRAIN_LAG):
+                if u % SEQ_UNITS == SEQ_UNITS - 1:
+                    score_max(u // SEQ_UNITS)
+            if slot >= QUANTISE_LAG:
                 quantise_data(slot - QUANTISE_LAG)
             for k in units_due(slot, EXP_LAG):
                 exponentials(k)
+            for k in units_due(slot, EXP_LAG + 1):
+                if k % SEQ_UNITS == SEQ_UNITS - 1:
+                    invert_sums(k // SEQ_UNITS)
             for k in units_due(slot, E_QUANTISE_LAG):
                 quantise_e(k)
-            for b in range(B):
-                if scale_slot(b) == slot:
-                    scale(b)
+            for b in range(B - 1):
+                if multiply_slot((b + 1) * SEQ_PASSES - 1) == slot:
+                    take_product(b, 0, nc.vector.tensor_copy)
+                    take_product(b, 1, nc.scalar.copy)
+                if multiply_slot((b + 1) * SEQ_PASSES - 1) + 1 == slot:
+                    take_mean(b, 0, True)
+                    take_mean(b, 1, False)
+                    store(b)
 
-        pooled = fin.tile([P, H], F32, name="pooled", bufs=1)
-        nc.vector.tensor_copy(out=pooled[:, 0:N_TILE], in_=mean_ps[0][:])
-        nc.scalar.copy(out=pooled[:, N_TILE:H], in_=mean_ps[1][:])
-        nc.sync.dma_start(out=out, in_=pooled[0:B, :])
+        quarters = parts(B - 1)
+        slot = LAST
+        for k in units_due(slot, E_QUANTISE_LAG):
+            copy_e(k)
+        quantise_data(LAST - 2)
+        regroup(LAST, quarters[0], 96)
+        for k in units_due(slot, E_QUANTISE_LAG):
+            quantise_e(k)
+        regroup(LAST, quarters[1], 96)
+        quantise_data(LAST - 1)
+        regroup(LAST, quarters[2], 96)
+        quantise_data(LAST, quarters[0])
+        regroup(LAST, quarters[3], 96)
+        for j in range(ALL_PASSES - 1):
+            if multiply_slot(j) >= slot:
+                for n in range(len(quarters)):
+                    multiply(j, n)
+        multiply(LAST, 0)
+        take_product(B - 1, 0, nc.scalar.copy)
+        for n in range(1, len(quarters)):
+            quantise_data(LAST, quarters[n])
+            multiply(LAST, n)
+            take_product(B - 1, n, nc.scalar.copy)
+            head_mean(B - 1, n - 1)
+        head_mean(B - 1, len(quarters) - 1)
+        for n in range(len(quarters)):
+            take_mean(B - 1, n, n % 2 == 1)
+        store(B - 1)

@@ -34,10 +34,10 @@ QUANTISE_LAG = 2
 MULTIPLY_LAG = 3
 SCORE_LAG = 1
 DRAIN_LAG = 2
-EXP_LAG = 7
-E_TRANSPOSE_LAG = 8
-E_QUANTISE_LAG = 9
-E_READY_LAG = 10
+E_TRANSPOSE_LAG = 1
+E_QUANTISE_LAG = 2
+E_READY_LAG = 3
+SUM_LAG = 2
 
 FLOPS = 2 * B * S * U * A + 2 * B * S * A * H
 
@@ -50,17 +50,31 @@ def units_due(slot, lag):
     return [u for u in range(ALL_UNITS) if unit_slot(u) + lag == slot]
 
 
+def exp_slot(u):
+    b, r = divmod(u, SEQ_UNITS)
+    return unit_slot(b * SEQ_UNITS + SEQ_UNITS - 1) + 3 + 3 * r // 2
+
+
+def exps_due(slot, lag):
+    return [u for u in range(ALL_UNITS) if exp_slot(u) + lag == slot]
+
+
 def multiply_slot(j):
-    return max(j + MULTIPLY_LAG, unit_slot(j // UNIT_PASSES) + E_READY_LAG)
+    return max(j + MULTIPLY_LAG, exp_slot(j // UNIT_PASSES) + E_READY_LAG)
 
 
 def vector_columns(i):
-    return 432 if i < EXP_LAG else 560
+    return 432 if i < exp_slot(0) else 568
+
+
+def mean_slot(b):
+    return max(multiply_slot((b + 1) * SEQ_PASSES - 1), unit_slot(ALL_UNITS - 1) + DRAIN_LAG) + 1
 
 
 def parts(b):
-    width = QUARTER if b == B - 1 else HALF
-    return [slice(h, h + width) for h in range(0, H, width)]
+    if b == B - 1:
+        return [slice(0, HALF), slice(HALF, HALF + QUARTER), slice(HALF + QUARTER, H)]
+    return [slice(0, HALF), slice(HALF, H)]
 
 
 def tile_selfattentionpooling_pa_kernel(tc, h_tanh, W2, padding_mask, data, out):
@@ -75,12 +89,14 @@ def tile_selfattentionpooling_pa_kernel(tc, h_tanh, W2, padding_mask, data, out)
         raw_pool = ctx.enter_context(tc.tile_pool(name="raw", bufs=4))
         grp_pool = ctx.enter_context(tc.tile_pool(name="grouped", bufs=4))
         d_keep = ctx.enter_context(tc.tile_pool(name="d_keep", bufs=10))
-        fin = ctx.enter_context(tc.tile_pool(name="fin", bufs=2))
+        fin = ctx.enter_context(tc.tile_pool(name="fin", bufs=B))
         psum = ctx.enter_context(tc.psum_pool(name="psum", bufs=1))
 
-        h_nat, scores, chunk_max, neg_max, e_T, sum_parts, inv_sum = ({} for n in range(7))
+        pieces = parts(B - 1)
+
+        h_nat, neg_scores, chunk_min, neg_max, e_T, sum_parts, col_sum = ({} for n in range(7))
         hT_ps, hT, l_ps, eW_ps, e_grouped = ({} for n in range(5))
-        raw, grouped, d_codes, d_scales, acc, attended, mean_ps, pooled = ({} for n in range(8))
+        raw, grouped, d_codes, d_scales, acc, attended, mean_ps = ({} for n in range(7))
 
         def load_data(i, cols=slice(0, H)):
             b, g = divmod(i, SEQ_PASSES)
@@ -143,25 +159,23 @@ def tile_selfattentionpooling_pa_kernel(tc, h_tanh, W2, padding_mask, data, out)
         def drain_scores(u):
             b, r = divmod(u, SEQ_UNITS)
             if r == 0:
-                scores[b] = seq_pool.tile([A, S], F32, name="scores")
-                chunk_max[b] = small.tile([A, SEQ_PASSES], F32, name="chunk_max")
+                neg_scores[b] = seq_pool.tile([A, S], F32, name="neg_scores")
+                chunk_min[b] = small.tile([A, SEQ_PASSES], F32, name="chunk_min")
             for cc in range(UNIT_PASSES):
                 c = r * UNIT_PASSES + cc
                 nc.vector.tensor_scalar(
-                    out=scores[b][:, c * K_PASS : (c + 1) * K_PASS].rearrange("a (p t) -> a p t", t=PACK),
+                    out=neg_scores[b][:, c * K_PASS : (c + 1) * K_PASS].rearrange("a (p t) -> a p t", t=PACK),
                     in0=l_ps[u, cc][:].rearrange("a t p -> a p t"),
-                    scalar1=1.0,
+                    scalar1=-1.0,
                     scalar2=None,
                     op0=ALU.mult,
-                    op1=ALU.max,
-                    accum_out=chunk_max[b][:, c : c + 1],
+                    op1=ALU.min,
+                    accum_out=chunk_min[b][:, c : c + 1],
                 )
 
-        def score_max(b):
-            col_max = small.tile([A, 1], F32, name="col_max")
-            nc.vector.tensor_reduce(out=col_max[:], in_=chunk_max[b][:], axis=AX.X, op=ALU.max)
+        def negative_max(b):
             neg_max[b] = small.tile([A, 1], F32, name="neg_max")
-            nc.vector.tensor_scalar_mul(out=neg_max[b][:], in0=col_max[:], scalar1=-1.0)
+            nc.vector.tensor_reduce(out=neg_max[b][:], in_=chunk_min[b][:], axis=AX.X, op=ALU.min)
 
         def exponentials(k):
             b, r = divmod(k, SEQ_UNITS)
@@ -171,10 +185,10 @@ def tile_selfattentionpooling_pa_kernel(tc, h_tanh, W2, padding_mask, data, out)
             cols = slice(r * UNIT, (r + 1) * UNIT)
             nc.scalar.activation(
                 out=e_T[b][:, cols],
-                in_=scores[b][:, cols],
+                in_=neg_scores[b][:, cols],
                 func=ACT.Exp,
                 bias=neg_max[b][:, 0:1],
-                scale=1.0,
+                scale=-1.0,
                 accum_out=sum_parts[b][:, r : r + 1],
             )
 
@@ -223,8 +237,7 @@ def tile_selfattentionpooling_pa_kernel(tc, h_tanh, W2, padding_mask, data, out)
             b, g = divmod(j, SEQ_PASSES)
             cols = parts(b)[n]
             if g == 0:
-                tag, bufs = ("l", 4) if b == B - 1 else ("acc%d" % n, 1)
-                acc[b, n] = psum.tile([A, cols.stop - cols.start], F32, tag=tag, bufs=bufs, name="acc")
+                acc[b, n] = psum.tile([A, cols.stop - cols.start], F32, tag=("acc0", "acc1", "hT")[n], name="acc")
             nc.tensor.matmul_mx(
                 out=acc[b, n][:],
                 lhsT=e_codes[:, j, :].bitcast(FP8X4),
@@ -235,11 +248,16 @@ def tile_selfattentionpooling_pa_kernel(tc, h_tanh, W2, padding_mask, data, out)
                 stop=(g == SEQ_PASSES - 1),
             )
 
+        def multiply_all(j):
+            for n in range(len(parts(j // SEQ_PASSES))):
+                multiply(j, n)
+
+        def add_sums(b):
+            col_sum[b] = small.tile([A, 1], F32, name="col_sum")
+            nc.vector.tensor_reduce(out=col_sum[b][:], in_=sum_parts[b][:], axis=AX.X, op=ALU.add)
+
         def invert_sums(b):
-            col_sum = small.tile([A, 1], F32, name="col_sum")
-            nc.vector.tensor_reduce(out=col_sum[:], in_=sum_parts[b][:], axis=AX.X, op=ALU.add)
-            inv_sum[b] = small.tile([A, 1], F32, name="inv_sum")
-            nc.vector.reciprocal(out=inv_sum[b][:], in_=col_sum[:])
+            nc.vector.reciprocal(out=mean_w[:, b, b : b + 1], in_=col_sum[b][:])
 
         def take_product(b, n, copy):
             if n == 0:
@@ -247,34 +265,24 @@ def tile_selfattentionpooling_pa_kernel(tc, h_tanh, W2, padding_mask, data, out)
             copy(out=attended[b][:, parts(b)[n]], in_=acc[b, n][:])
 
         def head_mean(b, n):
-            cols = parts(b)[n]
-            tag = ("acc0", "acc1", "hT", "eW")[n]
-            mean_ps[b, n] = psum.tile([P, cols.stop - cols.start], F32, tag=tag, name="mean_ps")
+            if b == 0:
+                mean_ps[n] = psum.tile([P, pieces[n].stop - pieces[n].start], F32, tag="l", bufs=4, name="mean_ps")
             nc.tensor.matmul(
-                out=mean_ps[b, n][:],
-                lhsT=inv_sum[b][:, 0:1].to_broadcast([A, P]),
-                rhs=attended[b][:, cols],
-                start=True,
-                stop=True,
+                out=mean_ps[n][:],
+                lhsT=mean_w[:, b, :],
+                rhs=attended[b][:, pieces[n]],
+                start=(b == 0),
+                stop=(b == B - 1),
             )
-
-        def take_mean(b, n, on_vector):
-            if n == 0:
-                pooled[b] = fin.tile([1, H], F32, name="pooled")
-            dst = pooled[b][:, parts(b)[n]]
-            if on_vector:
-                nc.vector.tensor_scalar_mul(out=dst, in0=mean_ps[b, n][0:1, :], scalar1=1.0 / A)
-            else:
-                nc.scalar.mul(dst, mean_ps[b, n][0:1, :], 1.0 / A)
-
-        def store(b):
-            nc.sync.dma_start(out=out[b : b + 1, :], in_=pooled[b][:])
 
         w2_sb = const.tile([U, A], BF16)
         nc.scalar.dma_start(out=w2_sb[:], in_=W2)
         mask_rows = const.tile([P, K_PASS], BF16)
         nc.vector.memset(mask_rows[:], 0.0)
         nc.scalar.dma_start(out=mask_rows[0:ALL_PASSES, :], in_=padding_mask.rearrange("b (c k) -> (b c) k", k=K_PASS))
+        warm = const.tile([P, 1], F32)
+        nc.gpsimd.memset(warm[:], 0.0)
+        nc.scalar.activation(out=warm[:], in_=warm[:], func=ACT.Exp)
         load_data(0, slice(0, HALF))
         load_data(0, slice(HALF, H))
         load_h(0)
@@ -286,6 +294,8 @@ def tile_selfattentionpooling_pa_kernel(tc, h_tanh, W2, padding_mask, data, out)
         make_identity(nc, ident_bf[:])
         ident_f32 = const.tile([P, P], F32)
         make_identity(nc, ident_f32[:])
+        mean_w = const.tile([A, B, P], F32)
+        nc.gpsimd.memset(mean_w[:], 0.0)
         pad_term = const.tile([P, ALL_PASSES, PACK], F32)
         e_codes = const.tile([P, ALL_PASSES, A], U32, align_bytes=64)
         e_scales = const.tile([P, ALL_PASSES, A], U8, align_bytes=64)
@@ -312,17 +322,12 @@ def tile_selfattentionpooling_pa_kernel(tc, h_tanh, W2, padding_mask, data, out)
 
             for u in units_due(slot, SCORE_LAG):
                 copy_hT(u)
-            for k in units_due(slot, E_QUANTISE_LAG):
+            for k in exps_due(slot, E_QUANTISE_LAG):
                 copy_e(k)
 
-            for b in range(B - 1):
-                if multiply_slot((b + 1) * SEQ_PASSES - 1) + 1 == slot:
-                    for n in range(len(parts(b))):
-                        head_mean(b, n)
             for j in range(ALL_PASSES):
                 if multiply_slot(j) == slot:
-                    for n in range(len(parts(j // SEQ_PASSES))):
-                        multiply(j, n)
+                    multiply_all(j)
             for u in units_due(slot, SCORE_LAG):
                 score_matmuls(u)
             if slot == 0:
@@ -335,59 +340,68 @@ def tile_selfattentionpooling_pa_kernel(tc, h_tanh, W2, padding_mask, data, out)
                 for u in units_due(slot, 0):
                     transpose_h(u)
                     padding_terms(u)
-            for k in units_due(slot, E_TRANSPOSE_LAG):
+            for k in exps_due(slot, E_TRANSPOSE_LAG):
                 transpose_e(k)
+            for b in range(B - 1):
+                if slot == mean_slot(b):
+                    for n in range(len(pieces)):
+                        head_mean(b, n)
 
             for u in units_due(slot, DRAIN_LAG):
                 drain_scores(u)
+            for k in exps_due(slot, SUM_LAG):
+                if k % SEQ_UNITS == SEQ_UNITS - 1:
+                    add_sums(k // SEQ_UNITS)
             if slot > 0:
                 regroup(slot, slice(0, H), vector_columns(slot))
-            for u in units_due(slot, DRAIN_LAG):
-                if u % SEQ_UNITS == SEQ_UNITS - 1:
-                    score_max(u // SEQ_UNITS)
-            if slot >= QUANTISE_LAG:
-                quantise_data(slot - QUANTISE_LAG)
-            for k in units_due(slot, EXP_LAG):
-                exponentials(k)
-            for k in units_due(slot, EXP_LAG + 1):
+            for k in exps_due(slot, SUM_LAG):
                 if k % SEQ_UNITS == SEQ_UNITS - 1:
                     invert_sums(k // SEQ_UNITS)
-            for k in units_due(slot, E_QUANTISE_LAG):
+            for u in units_due(slot, DRAIN_LAG):
+                if u % SEQ_UNITS == SEQ_UNITS - 1:
+                    negative_max(u // SEQ_UNITS)
+            for k in exps_due(slot, 0):
+                exponentials(k)
+            for k in exps_due(slot, E_QUANTISE_LAG):
                 quantise_e(k)
             for b in range(B - 1):
                 if multiply_slot((b + 1) * SEQ_PASSES - 1) == slot:
                     take_product(b, 0, nc.vector.tensor_copy)
                     take_product(b, 1, nc.scalar.copy)
-                if multiply_slot((b + 1) * SEQ_PASSES - 1) + 1 == slot:
-                    take_mean(b, 0, True)
-                    take_mean(b, 1, False)
-                    store(b)
 
-        quarters = parts(B - 1)
-        slot = LAST
-        for k in units_due(slot, E_QUANTISE_LAG):
-            copy_e(k)
+            if slot >= QUANTISE_LAG:
+                quantise_data(slot - QUANTISE_LAG)
+
+        for j in range(LAST - 2):
+            if multiply_slot(j) >= LAST:
+                multiply_all(j)
+        add_sums(B - 1)
         quantise_data(LAST - 2)
-        regroup(LAST, quarters[0], 96)
-        for k in units_due(slot, E_QUANTISE_LAG):
-            quantise_e(k)
-        regroup(LAST, quarters[1], 96)
+        multiply_all(LAST - 2)
+        invert_sums(B - 1)
+        copy_e(ALL_UNITS - 1)
+        regroup(LAST, pieces[0], 128)
+        quantise_e(ALL_UNITS - 1)
         quantise_data(LAST - 1)
-        regroup(LAST, quarters[2], 96)
-        quantise_data(LAST, quarters[0])
-        regroup(LAST, quarters[3], 96)
-        for j in range(ALL_PASSES - 1):
-            if multiply_slot(j) >= slot:
-                for n in range(len(quarters)):
-                    multiply(j, n)
+        multiply_all(LAST - 1)
+        regroup(LAST, pieces[1], 64)
+        quantise_data(LAST, pieces[0])
         multiply(LAST, 0)
+        regroup(LAST, pieces[2], 64)
         take_product(B - 1, 0, nc.scalar.copy)
-        for n in range(1, len(quarters)):
-            quantise_data(LAST, quarters[n])
-            multiply(LAST, n)
-            take_product(B - 1, n, nc.scalar.copy)
-            head_mean(B - 1, n - 1)
-        head_mean(B - 1, len(quarters) - 1)
-        for n in range(len(quarters)):
-            take_mean(B - 1, n, n % 2 == 1)
-        store(B - 1)
+        quantise_data(LAST, pieces[1])
+        multiply(LAST, 1)
+        quantise_data(LAST, pieces[2])
+        multiply(LAST, 2)
+        head_mean(B - 1, 0)
+        take_product(B - 1, 1, nc.scalar.copy)
+        take_product(B - 1, 2, nc.vector.tensor_copy)
+        head_mean(B - 1, 1)
+        head_mean(B - 1, 2)
+        pooled = fin.tile([B, H], F32, name="pooled", bufs=1)
+        for n in range(len(pieces)):
+            if n < 2:
+                nc.scalar.mul(pooled[:, pieces[n]], mean_ps[n][0:B, :], 1.0 / A)
+            else:
+                nc.vector.tensor_scalar_mul(out=pooled[:, pieces[n]], in0=mean_ps[n][0:B, :], scalar1=1.0 / A)
+        nc.sync.dma_start(out=out, in_=pooled[:])

@@ -64,11 +64,19 @@ def multiply_slot(j):
 
 
 def vector_columns(i):
-    return 432 if i < exp_slot(0) else 568
+    if i < exp_slot(0):
+        return 288 if gpsimd_columns(i) else 400
+    if i > unit_slot(ALL_UNITS - 1) + DRAIN_LAG:
+        return 624
+    return 352 if gpsimd_columns(i) else 528
+
+
+def gpsimd_columns(i):
+    return QUARTER if units_due(i, DRAIN_LAG) else 0
 
 
 def mean_slot(b):
-    return max(multiply_slot((b + 1) * SEQ_PASSES - 1), unit_slot(ALL_UNITS - 1) + DRAIN_LAG) + 1
+    return max(multiply_slot((b + 1) * SEQ_PASSES - 1) + 1, unit_slot(ALL_UNITS - 1) + DRAIN_LAG) + 1
 
 
 def parts(b):
@@ -88,6 +96,7 @@ def tile_selfattentionpooling_pa_kernel(tc, h_tanh, W2, padding_mask, data, out)
         small = ctx.enter_context(tc.tile_pool(name="small", bufs=B))
         raw_pool = ctx.enter_context(tc.tile_pool(name="raw", bufs=4))
         grp_pool = ctx.enter_context(tc.tile_pool(name="grouped", bufs=4))
+        g_pool = ctx.enter_context(tc.tile_pool(name="grouped_g", bufs=2))
         d_keep = ctx.enter_context(tc.tile_pool(name="d_keep", bufs=10))
         fin = ctx.enter_context(tc.tile_pool(name="fin", bufs=B))
         psum = ctx.enter_context(tc.psum_pool(name="psum", bufs=1))
@@ -96,7 +105,7 @@ def tile_selfattentionpooling_pa_kernel(tc, h_tanh, W2, padding_mask, data, out)
 
         h_nat, neg_scores, chunk_min, neg_max, e_T, sum_parts, col_sum = ({} for n in range(7))
         hT_ps, hT, l_ps, eW_ps, e_grouped = ({} for n in range(5))
-        raw, grouped, d_codes, d_scales, acc, attended, mean_ps = ({} for n in range(7))
+        raw, grouped, grouped_g, d_codes, d_scales, acc, attended, mean_ps = ({} for n in range(8))
 
         def load_data(i, cols=slice(0, H)):
             b, g = divmod(i, SEQ_PASSES)
@@ -213,6 +222,17 @@ def tile_selfattentionpooling_pa_kernel(tc, h_tanh, W2, padding_mask, data, out)
                 in_=e_grouped[k][:].rearrange("p g a j -> p (g a j)"),
             )
 
+        def regroup_gpsimd(i):
+            grouped_g[i] = g_pool.tile([P, QUARTER, PACK], BF16, name="grouped_g", align_bytes=64)
+            nc.gpsimd.tensor_scalar(
+                out=grouped_g[i][:].rearrange("p (c i) j -> p c j i", i=RUN),
+                in0=raw[i][:, :, H - QUARTER : H].rearrange("p j (c i) -> p c j i", i=RUN),
+                scalar1=1.0,
+                scalar2=0.0,
+                op0=ALU.mult,
+                op1=ALU.add,
+            )
+
         def regroup(i, cols, v_cols):
             if i not in grouped:
                 grouped[i] = grp_pool.tile([P, H, PACK], BF16, name="grouped", align_bytes=64)
@@ -227,11 +247,19 @@ def tile_selfattentionpooling_pa_kernel(tc, h_tanh, W2, padding_mask, data, out)
             if i not in d_codes:
                 d_codes[i] = d_keep.tile([P, H], U32, name="d_codes", align_bytes=64)
                 d_scales[i] = d_keep.tile([P, H], U8, name="d_scales", align_bytes=64)
-            nc.vector.quantize_mx(
-                out=d_codes[i][:, cols].bitcast(FP8X4),
-                scales=d_scales[i][:, cols],
-                in_=grouped[i][:, cols, :].rearrange("p h j -> p (h j)"),
-            )
+            runs = [(cols, grouped[i][:, cols, :])]
+            if i in grouped_g:
+                runs = [
+                    (slice(0, HALF), grouped[i][:, 0:HALF, :]),
+                    (slice(H - QUARTER, H), grouped_g[i][:]),
+                    (slice(HALF, H - QUARTER), grouped[i][:, HALF : H - QUARTER, :]),
+                ]
+            for run_cols, src in runs:
+                nc.vector.quantize_mx(
+                    out=d_codes[i][:, run_cols].bitcast(FP8X4),
+                    scales=d_scales[i][:, run_cols],
+                    in_=src.rearrange("p h j -> p (h j)"),
+                )
 
         def multiply(j, n):
             b, g = divmod(j, SEQ_PASSES)
@@ -349,11 +377,12 @@ def tile_selfattentionpooling_pa_kernel(tc, h_tanh, W2, padding_mask, data, out)
 
             for u in units_due(slot, DRAIN_LAG):
                 drain_scores(u)
+                regroup_gpsimd(slot)
             for k in exps_due(slot, SUM_LAG):
                 if k % SEQ_UNITS == SEQ_UNITS - 1:
                     add_sums(k // SEQ_UNITS)
             if slot > 0:
-                regroup(slot, slice(0, H), vector_columns(slot))
+                regroup(slot, slice(0, H - gpsimd_columns(slot)), vector_columns(slot))
             for k in exps_due(slot, SUM_LAG):
                 if k % SEQ_UNITS == SEQ_UNITS - 1:
                     invert_sums(k // SEQ_UNITS)
@@ -365,7 +394,7 @@ def tile_selfattentionpooling_pa_kernel(tc, h_tanh, W2, padding_mask, data, out)
             for k in exps_due(slot, E_QUANTISE_LAG):
                 quantise_e(k)
             for b in range(B - 1):
-                if multiply_slot((b + 1) * SEQ_PASSES - 1) == slot:
+                if multiply_slot((b + 1) * SEQ_PASSES - 1) + 1 == slot:
                     take_product(b, 0, nc.vector.tensor_copy)
                     take_product(b, 1, nc.scalar.copy)
 

@@ -35,15 +35,17 @@ MULTIPLY_LAG = 3
 SCORE_LAG = 1
 DRAIN_LAG = 2
 E_TRANSPOSE_LAG = 1
-E_QUANTISE_LAG = 2
-E_READY_LAG = 3
+E_COPY_LAG = 2
+E_QUANTISE_LAG = 3
+E_READY_LAG = 4
 SUM_LAG = 2
+EARLY = 1
 
 FLOPS = 2 * B * S * U * A + 2 * B * S * A * H
 
 
 def unit_slot(u):
-    return 3 * u // 2
+    return 3 * u // 2 - EARLY
 
 
 def units_due(slot, lag):
@@ -65,14 +67,14 @@ def multiply_slot(j):
 
 def vector_columns(i):
     if i < exp_slot(0):
-        return 288 if gpsimd_columns(i) else 400
+        return 288 if gpsimd_columns(i) else 528
     if i > unit_slot(ALL_UNITS - 1) + DRAIN_LAG:
-        return 624
-    return 352 if gpsimd_columns(i) else 528
+        return 592
+    return 352 if gpsimd_columns(i) else 544
 
 
 def gpsimd_columns(i):
-    return QUARTER if units_due(i, DRAIN_LAG) else 0
+    return QUARTER if i > 3 and units_due(i, DRAIN_LAG) else 0
 
 
 def mean_slot(b):
@@ -311,11 +313,12 @@ def tile_selfattentionpooling_pa_kernel(tc, h_tanh, W2, padding_mask, data, out)
         warm = const.tile([P, 1], F32)
         nc.gpsimd.memset(warm[:], 0.0)
         nc.scalar.activation(out=warm[:], in_=warm[:], func=ACT.Exp)
+        load_h(0)
         load_data(0, slice(0, HALF))
         load_data(0, slice(HALF, H))
-        load_h(0)
-        load_data(1)
         load_h(1)
+        load_data(1)
+        load_h(2)
         load_data(2)
 
         ident_bf = const.tile([P, P], BF16)
@@ -341,16 +344,22 @@ def tile_selfattentionpooling_pa_kernel(tc, h_tanh, W2, padding_mask, data, out)
                 op1=ALU.mult,
             )
 
+        transpose_h(0)
+        copy_hT(0)
+        regroup(0, slice(0, HALF), 256)
+        mask_terms()
+        padding_terms(0)
         for slot in range(ALL_PASSES - 1):
             if slot + LOAD_AHEAD < ALL_PASSES:
                 load_data(slot + LOAD_AHEAD)
             for u in units_due(slot, -H_AHEAD):
-                if u > 1:
+                if u > 2:
                     load_h(u)
 
             for u in units_due(slot, SCORE_LAG):
-                copy_hT(u)
-            for k in exps_due(slot, E_QUANTISE_LAG):
+                if u > 0:
+                    copy_hT(u)
+            for k in exps_due(slot, E_COPY_LAG):
                 copy_e(k)
 
             for j in range(ALL_PASSES):
@@ -359,15 +368,10 @@ def tile_selfattentionpooling_pa_kernel(tc, h_tanh, W2, padding_mask, data, out)
             for u in units_due(slot, SCORE_LAG):
                 score_matmuls(u)
             if slot == 0:
-                regroup(0, slice(0, HALF), 256)
                 regroup(0, slice(HALF, H), 256)
-                transpose_h(0)
-                mask_terms()
-                padding_terms(0)
-            else:
-                for u in units_due(slot, 0):
-                    transpose_h(u)
-                    padding_terms(u)
+            for u in units_due(slot, 0):
+                transpose_h(u)
+                padding_terms(u)
             for k in exps_due(slot, E_TRANSPOSE_LAG):
                 transpose_e(k)
             for b in range(B - 1):
@@ -377,7 +381,8 @@ def tile_selfattentionpooling_pa_kernel(tc, h_tanh, W2, padding_mask, data, out)
 
             for u in units_due(slot, DRAIN_LAG):
                 drain_scores(u)
-                regroup_gpsimd(slot)
+                if gpsimd_columns(slot):
+                    regroup_gpsimd(slot)
             for k in exps_due(slot, SUM_LAG):
                 if k % SEQ_UNITS == SEQ_UNITS - 1:
                     add_sums(k // SEQ_UNITS)
@@ -408,7 +413,6 @@ def tile_selfattentionpooling_pa_kernel(tc, h_tanh, W2, padding_mask, data, out)
         quantise_data(LAST - 2)
         multiply_all(LAST - 2)
         invert_sums(B - 1)
-        copy_e(ALL_UNITS - 1)
         regroup(LAST, pieces[0], 128)
         quantise_e(ALL_UNITS - 1)
         quantise_data(LAST - 1)

@@ -24,6 +24,7 @@ UNIT_PASSES = 2
 UNIT = UNIT_PASSES * K_PASS
 SEQ_UNITS = S // UNIT
 ALL_UNITS = B * SEQ_UNITS
+SCALAR_RUN = 8
 RUN = 4
 HALF = H // 2
 QUARTER = H // 4
@@ -239,10 +240,10 @@ def tile_selfattentionpooling_pa_kernel(tc, h_tanh, W2, padding_mask, data, out)
             if i not in grouped:
                 grouped[i] = grp_pool.tile([P, H, PACK], BF16, name="grouped", align_bytes=64)
             middle = cols.start + v_cols
-            for copy, h0, h1 in ((nc.vector.tensor_copy, cols.start, middle), (nc.scalar.copy, middle, cols.stop)):
+            for copy, h0, h1, run in ((nc.vector.tensor_copy, cols.start, middle, RUN), (nc.scalar.copy, middle, cols.stop, SCALAR_RUN)):
                 copy(
-                    out=grouped[i][:, h0:h1, :].rearrange("p (c i) j -> p c j i", i=RUN),
-                    in_=raw[i][:, :, h0:h1].rearrange("p j (c i) -> p c j i", i=RUN),
+                    out=grouped[i][:, h0:h1, :].rearrange("p (c i) j -> p c j i", i=run),
+                    in_=raw[i][:, :, h0:h1].rearrange("p j (c i) -> p c j i", i=run),
                 )
 
         def quantise_data(i, cols=slice(0, H)):
@@ -409,10 +410,8 @@ def tile_selfattentionpooling_pa_kernel(tc, h_tanh, W2, padding_mask, data, out)
         for j in range(LAST - 2):
             if multiply_slot(j) >= LAST:
                 multiply_all(j)
-        add_sums(B - 1)
         quantise_data(LAST - 2)
         multiply_all(LAST - 2)
-        invert_sums(B - 1)
         regroup(LAST, pieces[0], 128)
         quantise_e(ALL_UNITS - 1)
         quantise_data(LAST - 1)

@@ -24,8 +24,8 @@ UNIT_PASSES = 2
 UNIT = UNIT_PASSES * K_PASS
 SEQ_UNITS = S // UNIT
 ALL_UNITS = B * SEQ_UNITS
-SCALAR_RUN = 8
-RUN = 4
+GPSIMD_RUN = 4
+RUN = 8
 HALF = H // 2
 QUARTER = H // 4
 
@@ -228,8 +228,8 @@ def tile_selfattentionpooling_pa_kernel(tc, h_tanh, W2, padding_mask, data, out)
         def regroup_gpsimd(i):
             grouped_g[i] = g_pool.tile([P, QUARTER, PACK], BF16, name="grouped_g", align_bytes=64)
             nc.gpsimd.tensor_scalar(
-                out=grouped_g[i][:].rearrange("p (c i) j -> p c j i", i=RUN),
-                in0=raw[i][:, :, H - QUARTER : H].rearrange("p j (c i) -> p c j i", i=RUN),
+                out=grouped_g[i][:].rearrange("p (c i) j -> p c j i", i=GPSIMD_RUN),
+                in0=raw[i][:, :, H - QUARTER : H].rearrange("p j (c i) -> p c j i", i=GPSIMD_RUN),
                 scalar1=1.0,
                 scalar2=0.0,
                 op0=ALU.mult,
@@ -240,10 +240,10 @@ def tile_selfattentionpooling_pa_kernel(tc, h_tanh, W2, padding_mask, data, out)
             if i not in grouped:
                 grouped[i] = grp_pool.tile([P, H, PACK], BF16, name="grouped", align_bytes=64)
             middle = cols.start + v_cols
-            for copy, h0, h1, run in ((nc.vector.tensor_copy, cols.start, middle, RUN), (nc.scalar.copy, middle, cols.stop, SCALAR_RUN)):
+            for copy, h0, h1 in ((nc.vector.tensor_copy, cols.start, middle), (nc.scalar.copy, middle, cols.stop)):
                 copy(
-                    out=grouped[i][:, h0:h1, :].rearrange("p (c i) j -> p c j i", i=run),
-                    in_=raw[i][:, :, h0:h1].rearrange("p j (c i) -> p c j i", i=run),
+                    out=grouped[i][:, h0:h1, :].rearrange("p (c i) j -> p c j i", i=RUN),
+                    in_=raw[i][:, :, h0:h1].rearrange("p j (c i) -> p c j i", i=RUN),
                 )
 
         def quantise_data(i, cols=slice(0, H)):

@@ -68,10 +68,10 @@ def multiply_slot(j):
 
 def vector_columns(i):
     if i < exp_slot(0):
-        return 288 if gpsimd_columns(i) else 528
+        return 320 if gpsimd_columns(i) else 560
     if i > unit_slot(ALL_UNITS - 1) + DRAIN_LAG:
-        return 592
-    return 352 if gpsimd_columns(i) else 544
+        return 624
+    return 384 if gpsimd_columns(i) else 576
 
 
 def gpsimd_columns(i):

@@ -41,6 +41,14 @@ E_QUANTISE_LAG = 3
 E_READY_LAG = 4
 SUM_LAG = 2
 EARLY = 1
+VA = 304
+VB = 544
+VC = 368
+VD = 560
+VE = 608
+V_0 = 160
+V_1 = 96
+V_2 = 160
 
 FLOPS = 2 * B * S * U * A + 2 * B * S * A * H
 
@@ -68,10 +76,10 @@ def multiply_slot(j):
 
 def vector_columns(i):
     if i < exp_slot(0):
-        return 320 if gpsimd_columns(i) else 560
+        return VA if gpsimd_columns(i) else VB
     if i > unit_slot(ALL_UNITS - 1) + DRAIN_LAG:
-        return 624
-    return 384 if gpsimd_columns(i) else 576
+        return VE
+    return VC if gpsimd_columns(i) else VD
 
 
 def gpsimd_columns(i):
@@ -350,7 +358,7 @@ def tile_selfattentionpooling_pa_kernel(tc, h_tanh, W2, padding_mask, data, out)
         regroup(0, slice(0, HALF), 256)
         mask_terms()
         padding_terms(0)
-        for slot in range(ALL_PASSES - 1):
+        for slot in range(ALL_PASSES - 2):
             if slot + LOAD_AHEAD < ALL_PASSES:
                 load_data(slot + LOAD_AHEAD)
             for u in units_due(slot, -H_AHEAD):
@@ -407,28 +415,48 @@ def tile_selfattentionpooling_pa_kernel(tc, h_tanh, W2, padding_mask, data, out)
             if slot >= QUANTISE_LAG:
                 quantise_data(slot - QUANTISE_LAG)
 
-        for j in range(LAST - 2):
-            if multiply_slot(j) >= LAST:
+        ends = (LAST - 1, LAST)
+
+        def regroup_ends(n, v_cols):
+            for i in ends:
+                regroup(i, pieces[n], v_cols)
+
+        def quantise_ends(n):
+            for i in ends:
+                quantise_data(i, pieces[n])
+
+        def multiply_ends(n):
+            for i in ends:
+                multiply(i, n)
+
+        last_unit = ALL_UNITS - 1
+        for j in range(LAST - 3):
+            if multiply_slot(j) >= LAST - 1:
                 multiply_all(j)
+        copy_e(last_unit)
+        add_sums(B - 1)
+        quantise_e(last_unit - 1)
+        regroup_ends(0, V_0)
+        invert_sums(B - 1)
+        quantise_data(LAST - 3)
+        multiply_all(LAST - 3)
+        quantise_e(last_unit)
         quantise_data(LAST - 2)
         multiply_all(LAST - 2)
-        regroup(LAST, pieces[0], 128)
-        quantise_e(ALL_UNITS - 1)
-        quantise_data(LAST - 1)
-        multiply_all(LAST - 1)
-        regroup(LAST, pieces[1], 64)
-        quantise_data(LAST, pieces[0])
-        multiply(LAST, 0)
-        regroup(LAST, pieces[2], 64)
+        regroup_ends(1, V_1)
+        quantise_ends(0)
+        multiply_ends(0)
+        regroup(LAST - 1, pieces[2], V_2)
+        quantise_ends(1)
+        multiply_ends(1)
         take_product(B - 1, 0, nc.scalar.copy)
-        quantise_data(LAST, pieces[1])
-        multiply(LAST, 1)
-        quantise_data(LAST, pieces[2])
-        multiply(LAST, 2)
+        regroup(LAST, pieces[2], V_2)
         head_mean(B - 1, 0)
+        quantise_ends(2)
         take_product(B - 1, 1, nc.scalar.copy)
-        take_product(B - 1, 2, nc.vector.tensor_copy)
+        multiply_ends(2)
         head_mean(B - 1, 1)
+        take_product(B - 1, 2, nc.vector.tensor_copy)
         head_mean(B - 1, 2)
         pooled = fin.tile([B, H], F32, name="pooled", bufs=1)
         for n in range(len(pieces)):

@@ -371,18 +371,19 @@ def tile_selfattentionpooling_pa_kernel(tc, h_tanh, W2, padding_mask, data, out)
             for k in exps_due(slot, E_COPY_LAG):
                 copy_e(k)
 
+            if slot == 0:
+                regroup(0, slice(HALF, H), 256)
+            for u in units_due(slot, SCORE_LAG):
+                score_matmuls(u)
+            for u in units_due(slot, 0):
+                transpose_h(u)
+            for k in exps_due(slot, E_TRANSPOSE_LAG):
+                transpose_e(k)
+            for u in units_due(slot, 0):
+                padding_terms(u)
             for j in range(ALL_PASSES):
                 if multiply_slot(j) == slot:
                     multiply_all(j)
-            for u in units_due(slot, SCORE_LAG):
-                score_matmuls(u)
-            if slot == 0:
-                regroup(0, slice(HALF, H), 256)
-            for u in units_due(slot, 0):
-                transpose_h(u)
-                padding_terms(u)
-            for k in exps_due(slot, E_TRANSPOSE_LAG):
-                transpose_e(k)
             for b in range(B - 1):
                 if slot == mean_slot(b):
                     for n in range(len(pieces)):

from contextlib import ExitStack

import concourse.mybir as mybir
from concourse.masks import make_identity

BF16 = mybir.dt.bfloat16
F32 = mybir.dt.float32
U32 = mybir.dt.uint32
U8 = mybir.dt.uint8
FP8X4 = mybir.dt.float8_e4m3fn_x4
ALU = mybir.AluOpType
ACT = mybir.ActivationFunctionType
AX = mybir.AxisListType

B, S, H, U, A = 4, 4096, 1024, 128, 128
P = 128
PACK = 4
K_PASS = P * PACK
SEQ_PASSES = S // K_PASS
ALL_PASSES = B * SEQ_PASSES
LAST = ALL_PASSES - 1
NEG = -1e20
UNIT_PASSES = 2
UNIT = UNIT_PASSES * K_PASS
SEQ_UNITS = S // UNIT
ALL_UNITS = B * SEQ_UNITS
GPSIMD_RUN = 4
RUN = 8
HALF = H // 2
QUARTER = H // 4

LOAD_AHEAD = 3
H_AHEAD = 3
QUANTISE_LAG = 2
MULTIPLY_LAG = 3
SCORE_LAG = 1
DRAIN_LAG = 2
E_TRANSPOSE_LAG = 1
E_COPY_LAG = 2
E_QUANTISE_LAG = 3
E_READY_LAG = 4
SUM_LAG = 2
EARLY = 1
VA = 304
VB = 544
VC = 368
VD = 560
VE = 608
V_0 = 160
V_1 = 96
V_2 = 160

FLOPS = 2 * B * S * U * A + 2 * B * S * A * H


def unit_slot(u):
    return 3 * u // 2 - EARLY


def units_due(slot, lag):
    return [u for u in range(ALL_UNITS) if unit_slot(u) + lag == slot]


def exp_slot(u):
    b, r = divmod(u, SEQ_UNITS)
    return unit_slot(b * SEQ_UNITS + SEQ_UNITS - 1) + 3 + 3 * r // 2


def exps_due(slot, lag):
    return [u for u in range(ALL_UNITS) if exp_slot(u) + lag == slot]


def multiply_slot(j):
    return max(j + MULTIPLY_LAG, exp_slot(j // UNIT_PASSES) + E_READY_LAG)


def vector_columns(i):
    if i < exp_slot(0):
        return VA if gpsimd_columns(i) else VB
    if i > unit_slot(ALL_UNITS - 1) + DRAIN_LAG:
        return VE
    return VC if gpsimd_columns(i) else VD


def gpsimd_columns(i):
    return QUARTER if i > 3 and units_due(i, DRAIN_LAG) else 0


def mean_slot(b):
    return max(multiply_slot((b + 1) * SEQ_PASSES - 1) + 1, unit_slot(ALL_UNITS - 1) + DRAIN_LAG) + 1


def parts(b):
    if b == B - 1:
        return [slice(0, HALF), slice(HALF, HALF + QUARTER), slice(HALF + QUARTER, H)]
    return [slice(0, HALF), slice(HALF, H)]


def tile_selfattentionpooling_pa_kernel(tc, h_tanh, W2, padding_mask, data, out):
    nc = tc.nc
    with ExitStack() as ctx:
        ctx.enter_context(tc.manual_schedule())
        const = ctx.enter_context(tc.tile_pool(name="const", bufs=1))
        h_pool = ctx.enter_context(tc.tile_pool(name="h", bufs=5))
        stage = ctx.enter_context(tc.tile_pool(name="stage", bufs=2))
        seq_pool = ctx.enter_context(tc.tile_pool(name="seq", bufs=2))
        small = ctx.enter_context(tc.tile_pool(name="small", bufs=B))
        raw_pool = ctx.enter_context(tc.tile_pool(name="raw", bufs=4))
        grp_pool = ctx.enter_context(tc.tile_pool(name="grouped", bufs=4))
        g_pool = ctx.enter_context(tc.tile_pool(name="grouped_g", bufs=2))
        d_keep = ctx.enter_context(tc.tile_pool(name="d_keep", bufs=10))
        fin = ctx.enter_context(tc.tile_pool(name="fin", bufs=B))
        psum = ctx.enter_context(tc.psum_pool(name="psum", bufs=1))

        pieces = parts(B - 1)

        h_nat, neg_scores, chunk_min, neg_max, e_T, sum_parts, col_sum = ({} for n in range(7))
        hT_ps, hT, l_ps, eW_ps, e_grouped = ({} for n in range(5))
        raw, grouped, grouped_g, d_codes, d_scales, acc, attended, mean_ps = ({} for n in range(8))

        def load_data(i, cols=slice(0, H)):
            b, g = divmod(i, SEQ_PASSES)
            if i not in raw:
                raw[i] = raw_pool.tile([P, PACK, H], BF16, name="raw")
            src = data[b, g * K_PASS : (g + 1) * K_PASS, :]
            if cols == slice(0, H):
                nc.sync.dma_start(
                    out=raw[i][:].rearrange("p (u e) h -> p u (e h)", e=2),
                    in_=src.rearrange("(u p e) h -> p u (e h)", u=2, e=2),
                )
            else:
                for u in range(2):
                    nc.sync.dma_start(
                        out=raw[i][:, 2 * u : 2 * u + 2, cols],
                        in_=src.rearrange("(u p e) h -> u p e h", u=2, e=2)[u, :, :, cols],
                    )

        def load_h(u):
            b, r = divmod(u, SEQ_UNITS)
            h_nat[u] = h_pool.tile([P, UNIT_PASSES, PACK, U], BF16, name="h_nat")
            nc.sync.dma_start(
                out=h_nat[u][:].rearrange("p c t u -> p c (t u)"),
                in_=h_tanh[b, r * UNIT : (r + 1) * UNIT, :].rearrange("(c p t) u -> p c (t u)", p=P, t=PACK),
            )

        def transpose_h(u):
            hT_ps[u] = psum.tile([U, UNIT_PASSES, PACK, P], BF16, tag="hT", name="hT_ps")
            for cc in range(UNIT_PASSES):
                for t in range(PACK):
                    nc.tensor.transpose(hT_ps[u][:, cc, t, :], h_nat[u][:, cc, t, :], ident_bf[:])

        def padding_terms(u):
            for cc in range(UNIT_PASSES):
                l_ps[u, cc] = psum.tile([A, PACK, P], F32, tag="l", bufs=4, name="l_ps")
                for t in range(PACK):
                    nc.tensor.matmul(
                        out=l_ps[u, cc][:, t, :],
                        lhsT=pad_term[:, u * UNIT_PASSES + cc, t : t + 1].to_broadcast([P, A]),
                        rhs=ident_f32[:],
                        is_transpose=True,
                        start=(t == 0),
                        stop=False,
                    )

        def copy_hT(u):
            hT[u] = stage.tile([U, UNIT_PASSES, PACK, P], BF16, name="hT")
            nc.scalar.copy(out=hT[u][:], in_=hT_ps[u][:])

        def score_matmuls(u):
            for cc in range(UNIT_PASSES):
                nc.tensor.matmul(
                    out=l_ps[u, cc][:].rearrange("a t p -> a (t p)"),
                    lhsT=w2_sb[:],
                    rhs=hT[u][:, cc, :, :].rearrange("u t p -> u (t p)"),
                    start=False,
                    stop=True,
                )

        def drain_scores(u):
            b, r = divmod(u, SEQ_UNITS)
            if r == 0:
                neg_scores[b] = seq_pool.tile([A, S], F32, name="neg_scores")
                chunk_min[b] = small.tile([A, SEQ_PASSES], F32, name="chunk_min")
            for cc in range(UNIT_PASSES):
                c = r * UNIT_PASSES + cc
                nc.vector.tensor_scalar(
                    out=neg_scores[b][:, c * K_PASS : (c + 1) * K_PASS].rearrange("a (p t) -> a p t", t=PACK),
                    in0=l_ps[u, cc][:].rearrange("a t p -> a p t"),
                    scalar1=-1.0,
                    scalar2=None,
                    op0=ALU.mult,
                    op1=ALU.min,
                    accum_out=chunk_min[b][:, c : c + 1],
                )

        def negative_max(b):
            neg_max[b] = small.tile([A, 1], F32, name="neg_max")
            nc.vector.tensor_reduce(out=neg_max[b][:], in_=chunk_min[b][:], axis=AX.X, op=ALU.min)

        def exponentials(k):
            b, r = divmod(k, SEQ_UNITS)
            if r == 0:
                e_T[b] = seq_pool.tile([A, S], BF16, name="e_T")
                sum_parts[b] = small.tile([A, SEQ_UNITS], F32, name="sum_parts")
            cols = slice(r * UNIT, (r + 1) * UNIT)
            nc.scalar.activation(
                out=e_T[b][:, cols],
                in_=neg_scores[b][:, cols],
                func=ACT.Exp,
                bias=neg_max[b][:, 0:1],
                scale=-1.0,
                accum_out=sum_parts[b][:, r : r + 1],
            )

        def transpose_e(k):
            b, r = divmod(k, SEQ_UNITS)
            e_words = e_T[b][:].bitcast(F32)
            eW_ps[k] = psum.tile([P, UNIT_PASSES, 2, A], F32, tag="eW", name="eW_ps")
            for gg in range(UNIT_PASSES):
                for u in range(2):
                    w0 = ((r * UNIT_PASSES + gg) * 2 + u) * P
                    nc.tensor.transpose(eW_ps[k][:, gg, u, :], e_words[:, w0 : w0 + P], ident_f32[:])

        def copy_e(k):
            e_grouped[k] = stage.tile([P, UNIT_PASSES, A, PACK], BF16, name="e_grouped", align_bytes=64)
            nc.scalar.copy(out=e_grouped[k][:].bitcast(F32), in_=eW_ps[k][:].rearrange("p g u a -> p g a u"))

        def quantise_e(k):
            passes = slice(k * UNIT_PASSES, (k + 1) * UNIT_PASSES)
            nc.vector.quantize_mx(
                out=e_codes[:, passes, :].rearrange("p g a -> p (g a)").bitcast(FP8X4),
                scales=e_scales[:, passes, :].rearrange("p g a -> p (g a)"),
                in_=e_grouped[k][:].rearrange("p g a j -> p (g a j)"),
            )

        def regroup_gpsimd(i):
            grouped_g[i] = g_pool.tile([P, QUARTER, PACK], BF16, name="grouped_g", align_bytes=64)
            nc.gpsimd.tensor_scalar(
                out=grouped_g[i][:].rearrange("p (c i) j -> p c j i", i=GPSIMD_RUN),
                in0=raw[i][:, :, H - QUARTER : H].rearrange("p j (c i) -> p c j i", i=GPSIMD_RUN),
                scalar1=1.0,
                scalar2=0.0,
                op0=ALU.mult,
                op1=ALU.add,
            )

        def regroup(i, cols, v_cols):
            if i not in grouped:
                grouped[i] = grp_pool.tile([P, H, PACK], BF16, name="grouped", align_bytes=64)
            middle = cols.start + v_cols
            for copy, h0, h1 in ((nc.vector.tensor_copy, cols.start, middle), (nc.scalar.copy, middle, cols.stop)):
                copy(
                    out=grouped[i][:, h0:h1, :].rearrange("p (c i) j -> p c j i", i=RUN),
                    in_=raw[i][:, :, h0:h1].rearrange("p j (c i) -> p c j i", i=RUN),
                )

        def quantise_data(i, cols=slice(0, H)):
            if i not in d_codes:
                d_codes[i] = d_keep.tile([P, H], U32, name="d_codes", align_bytes=64)
                d_scales[i] = d_keep.tile([P, H], U8, name="d_scales", align_bytes=64)
            runs = [(cols, grouped[i][:, cols, :])]
            if i in grouped_g:
                runs = [
                    (slice(0, HALF), grouped[i][:, 0:HALF, :]),
                    (slice(H - QUARTER, H), grouped_g[i][:]),
                    (slice(HALF, H - QUARTER), grouped[i][:, HALF : H - QUARTER, :]),
                ]
            for run_cols, src in runs:
                nc.vector.quantize_mx(
                    out=d_codes[i][:, run_cols].bitcast(FP8X4),
                    scales=d_scales[i][:, run_cols],
                    in_=src.rearrange("p h j -> p (h j)"),
                )

        def multiply(j, n):
            b, g = divmod(j, SEQ_PASSES)
            cols = parts(b)[n]
            if g == 0:
                acc[b, n] = psum.tile([A, cols.stop - cols.start], F32, tag=("acc0", "acc1", "hT")[n], name="acc")
            nc.tensor.matmul_mx(
                out=acc[b, n][:],
                lhsT=e_codes[:, j, :].bitcast(FP8X4),
                lhsT_scale=e_scales[:, j, :],
                rhs=d_codes[j][:, cols].bitcast(FP8X4),
                rhs_scale=d_scales[j][:, cols],
                start=(g == 0),
                stop=(g == SEQ_PASSES - 1),
            )

        def multiply_all(j):
            for n in range(len(parts(j // SEQ_PASSES))):
                multiply(j, n)

        def add_sums(b):
            col_sum[b] = small.tile([A, 1], F32, name="col_sum")
            nc.vector.tensor_reduce(out=col_sum[b][:], in_=sum_parts[b][:], axis=AX.X, op=ALU.add)

        def invert_sums(b):
            nc.vector.reciprocal(out=mean_w[:, b, b : b + 1], in_=col_sum[b][:])

        def take_product(b, n, copy):
            if n == 0:
                attended[b] = fin.tile([A, H], F32, name="attended")
            copy(out=attended[b][:, parts(b)[n]], in_=acc[b, n][:])

        def head_mean(b, n):
            if b == 0:
                mean_ps[n] = psum.tile([P, pieces[n].stop - pieces[n].start], F32, tag="l", bufs=4, name="mean_ps")
            nc.tensor.matmul(
                out=mean_ps[n][:],
                lhsT=mean_w[:, b, :],
                rhs=attended[b][:, pieces[n]],
                start=(b == 0),
                stop=(b == B - 1),
            )

        w2_sb = const.tile([U, A], BF16)
        nc.scalar.dma_start(out=w2_sb[:], in_=W2)
        mask_rows = const.tile([P, K_PASS], BF16)
        nc.vector.memset(mask_rows[:], 0.0)
        nc.scalar.dma_start(out=mask_rows[0:ALL_PASSES, :], in_=padding_mask.rearrange("b (c k) -> (b c) k", k=K_PASS))
        warm = const.tile([P, 1], F32)
        nc.gpsimd.memset(warm[:], 0.0)
        nc.scalar.activation(out=warm[:], in_=warm[:], func=ACT.Exp)
        load_h(0)
        load_data(0, slice(0, HALF))
        load_data(0, slice(HALF, H))
        load_h(1)
        load_data(1)
        load_h(2)
        load_data(2)

        ident_bf = const.tile([P, P], BF16)
        make_identity(nc, ident_bf[:])
        ident_f32 = const.tile([P, P], F32)
        make_identity(nc, ident_f32[:])
        mean_w = const.tile([A, B, P], F32)
        nc.gpsimd.memset(mean_w[:], 0.0)
        pad_term = const.tile([P, ALL_PASSES, PACK], F32)
        e_codes = const.tile([P, ALL_PASSES, A], U32, align_bytes=64)
        e_scales = const.tile([P, ALL_PASSES, A], U8, align_bytes=64)

        def mask_terms():
            mask_ps = psum.tile([P, PACK, P], BF16, tag="eW", name="mask_ps")
            for t in range(PACK):
                nc.tensor.transpose(mask_ps[:, t, :], mask_rows[:].rearrange("r (p t) -> r t p", t=PACK)[:, t, :], ident_bf[:])
            nc.vector.tensor_scalar(
                out=pad_term[:],
                in0=mask_ps[:, :, 0:ALL_PASSES].rearrange("p t r -> p r t"),
                scalar1=1.0,
                scalar2=-NEG,
                op0=ALU.subtract,
                op1=ALU.mult,
            )

        transpose_h(0)
        copy_hT(0)
        regroup(0, slice(0, HALF), 256)
        mask_terms()
        padding_terms(0)
        for slot in range(ALL_PASSES - 2):
            if slot + LOAD_AHEAD < ALL_PASSES:
                load_data(slot + LOAD_AHEAD)
            for u in units_due(slot, -H_AHEAD):
                if u > 2:
                    load_h(u)

            for u in units_due(slot, SCORE_LAG):
                if u > 0:
                    copy_hT(u)
            for k in exps_due(slot, E_COPY_LAG):
                copy_e(k)

            if slot == 0:
                regroup(0, slice(HALF, H), 256)
            for u in units_due(slot, SCORE_LAG):
                score_matmuls(u)
            for u in units_due(slot, 0):
                transpose_h(u)
            for k in exps_due(slot, E_TRANSPOSE_LAG):
                transpose_e(k)
            for u in units_due(slot, 0):
                padding_terms(u)
            for j in range(ALL_PASSES):
                if multiply_slot(j) == slot:
                    multiply_all(j)
            for b in range(B - 1):
                if slot == mean_slot(b):
                    for n in range(len(pieces)):
                        head_mean(b, n)

            for u in units_due(slot, DRAIN_LAG):
                drain_scores(u)
                if gpsimd_columns(slot):
                    regroup_gpsimd(slot)
            for k in exps_due(slot, SUM_LAG):
                if k % SEQ_UNITS == SEQ_UNITS - 1:
                    add_sums(k // SEQ_UNITS)
            if slot > 0:
                regroup(slot, slice(0, H - gpsimd_columns(slot)), vector_columns(slot))
            for k in exps_due(slot, SUM_LAG):
                if k % SEQ_UNITS == SEQ_UNITS - 1:
                    invert_sums(k // SEQ_UNITS)
            for u in units_due(slot, DRAIN_LAG):
                if u % SEQ_UNITS == SEQ_UNITS - 1:
                    negative_max(u // SEQ_UNITS)
            for k in exps_due(slot, 0):
                exponentials(k)
            for k in exps_due(slot, E_QUANTISE_LAG):
                quantise_e(k)
            for b in range(B - 1):
                if multiply_slot((b + 1) * SEQ_PASSES - 1) + 1 == slot:
                    take_product(b, 0, nc.vector.tensor_copy)
                    take_product(b, 1, nc.scalar.copy)

            if slot >= QUANTISE_LAG:
                quantise_data(slot - QUANTISE_LAG)

        ends = (LAST - 1, LAST)

        def regroup_ends(n, v_cols):
            for i in ends:
                regroup(i, pieces[n], v_cols)

        def quantise_ends(n):
            for i in ends:
                quantise_data(i, pieces[n])

        def multiply_ends(n):
            for i in ends:
                multiply(i, n)

        last_unit = ALL_UNITS - 1
        for j in range(LAST - 3):
            if multiply_slot(j) >= LAST - 1:
                multiply_all(j)
        copy_e(last_unit)
        add_sums(B - 1)
        quantise_e(last_unit - 1)
        regroup_ends(0, V_0)
        invert_sums(B - 1)
        quantise_data(LAST - 3)
        multiply_all(LAST - 3)
        quantise_e(last_unit)
        quantise_data(LAST - 2)
        multiply_all(LAST - 2)
        regroup_ends(1, V_1)
        quantise_ends(0)
        multiply_ends(0)
        regroup(LAST - 1, pieces[2], V_2)
        quantise_ends(1)
        multiply_ends(1)
        take_product(B - 1, 0, nc.scalar.copy)
        regroup(LAST, pieces[2], V_2)
        head_mean(B - 1, 0)
        quantise_ends(2)
        take_product(B - 1, 1, nc.scalar.copy)
        multiply_ends(2)
        head_mean(B - 1, 1)
        take_product(B - 1, 2, nc.vector.tensor_copy)
        head_mean(B - 1, 2)
        pooled = fin.tile([B, H], F32, name="pooled", bufs=1)
        for n in range(len(pieces)):
            if n < 2:
                nc.scalar.mul(pooled[:, pieces[n]], mean_ps[n][0:B, :], 1.0 / A)
            else:
                nc.vector.tensor_scalar_mul(out=pooled[:, pieces[n]], in0=mean_ps[n][0:B, :], scalar1=1.0 / A)
        nc.sync.dma_start(out=out, in_=pooled[:])
